import numpy as np
import ml_dtypes


def mxq(x, axis, fmt="e4m3"):
    dtype, down = {"e4m3": (ml_dtypes.float8_e4m3fn, 7), "e5m2": (ml_dtypes.float8_e5m2, 14)}[fmt]
    v = np.moveaxis(np.asarray(x, np.float32).astype(ml_dtypes.bfloat16).astype(np.float64), axis, -1)
    blocks = v.reshape(v.shape[:-1] + (-1, 32))
    amax = np.abs(blocks).max(-1, keepdims=True)
    byte = np.maximum(np.where(amax > 0, np.frexp(amax)[1] - 1 + 127, 0) - down, 1)
    scale = np.exp2(byte - 127.0)
    codes = (blocks / scale).astype(np.float32).astype(dtype).astype(np.float64)
    return np.moveaxis((codes * scale).reshape(v.shape), -1, axis)


WIDE = False


def mx_kscale(k):
    if not WIDE:
        return np.ones(k)
    levels = np.array([10, -10, 5, -5, 0])
    a = np.random.permutation(np.resize(levels, k // 512 * 4)).reshape(k // 512, 4)
    idx = np.arange(k)
    return np.exp2(a[idx // 512, idx % 128 // 32])


BF16 = ml_dtypes.bfloat16


def bf(x):
    return np.asarray(x, np.float32).astype(BF16)


def f64(x):
    return np.asarray(x).astype(np.float64)


B, N, F_IN, F_HID, F_OUT = 8, 1024, 512, 128, 512


def normalize_adj(adj):
    colsum = adj.sum(axis=1)
    safe = np.where(colsum > 0, colsum, 1.0)
    r = np.where(colsum > 0, safe ** -0.5, 0.0)
    return r[:, :, None] * adj.transpose(0, 2, 1) * r[:, None, :]


def setup_inputs():
    s = mx_kscale(F_IN)
    keep = np.random.random((B, 1, N)) >= 0.05
    return {"batch_graph": bf(np.random.standard_normal((B, N, F_IN)) * s),
            "adj": bf(np.random.random((B, N, N)) * keep),
            "W1": bf(np.random.standard_normal((F_IN, F_HID)) * 0.3 * np.sqrt(N / F_IN) / s[:, None]),
            "b1": bf(np.random.standard_normal(F_HID) * 0.2)}


def reference(batch_graph, adj, W1, b1):
    a = normalize_adj(f64(adj))
    h = mxq(f64(batch_graph), 2, "e4m3") @ mxq(f64(W1), 0, "e4m3")
    y = (mxq(a, 2, "e4m3") @ mxq(h, 1, "e4m3")) + f64(b1)
    return np.maximum(y, 0.0)

@@ -1,0 +1,230 @@
+from contextlib import ExitStack
+
+import concourse.mybir as mybir
+from concourse.masks import make_identity
+
+F32 = mybir.dt.float32
+BF16 = mybir.dt.bfloat16
+U32 = mybir.dt.uint32
+U8 = mybir.dt.uint8
+FP8X4 = mybir.dt.float8_e4m3fn_x4
+ALU = mybir.AluOpType
+ACT = mybir.ActivationFunctionType
+
+P = 128
+G = 8
+N = 1024
+FI = 512
+FH = 128
+NB = N // P
+FLOPS = 2 * G * N * FI * FH + 2 * G * N * N * FH
+
+A_ON_VECTOR = (7,)
+
+
+def tile_gcn_pa_t_kernel(tc, batch_graph, adj, W1, b1, out):
+    nc = tc.nc
+    with ExitStack() as ctx:
+        const = ctx.enter_context(tc.tile_pool(name="const", bufs=1))
+        apool = ctx.enter_context(tc.tile_pool(name="apool", bufs=3))
+        xpool = ctx.enter_context(tc.tile_pool(name="xpool", bufs=3))
+        xgpool = ctx.enter_context(tc.tile_pool(name="xgpool", bufs=2))
+        t1pool = ctx.enter_context(tc.tile_pool(name="t1pool", bufs=3))
+        agpool = ctx.enter_context(tc.tile_pool(name="agpool", bufs=4))
+        acpool = ctx.enter_context(tc.tile_pool(name="acpool", bufs=8))
+        hpool = ctx.enter_context(tc.tile_pool(name="hpool", bufs=2))
+        small = ctx.enter_context(tc.tile_pool(name="small", bufs=3))
+        opool = ctx.enter_context(tc.tile_pool(name="opool", bufs=4))
+        ps_xt = ctx.enter_context(tc.psum_pool(name="ps_xt", bufs=2))
+        ps_h = ctx.enter_context(tc.psum_pool(name="ps_h", bufs=1))
+        ps_cs = ctx.enter_context(tc.psum_pool(name="ps_cs", bufs=1))
+        ps_r = ctx.enter_context(tc.psum_pool(name="ps_r", bufs=1))
+        ps_o = ctx.enter_context(tc.psum_pool(name="ps_o", bufs=2))
+
+        ident = const.tile([P, P], F32)
+        make_identity(nc, ident[:])
+        ones = const.tile([P, 2], BF16)
+        nc.vector.memset(ones[:], 1.0)
+        warm = const.tile([P, 1], F32)
+        nc.vector.memset(warm[:], 1.0)
+        nc.scalar.activation(out=warm[:], in_=warm[:], func=ACT.Sqrt)
+
+        w_raw = const.tile([P, 4, FH], BF16)
+        nc.scalar.dma_start(
+            out=w_raw[:].rearrange("q (u e) f -> q u (e f)", u=2),
+            in_=W1.rearrange("(u q e) f -> q u (e f)", u=2, e=2),
+        )
+        b_bf = const.tile([P, FH], BF16)
+        nc.scalar.dma_start(out=b_bf[:], in_=b1.partition_broadcast(P))
+        w_grp = const.tile([P, FH, 4], BF16, align_bytes=64)
+        nc.vector.tensor_copy(out=w_grp[:], in_=w_raw[:].rearrange("q t f -> q f t"))
+        b_f = const.tile([P, FH], F32)
+        nc.vector.tensor_copy(out=b_f[:], in_=b_bf[:])
+        w_c = const.tile([P, FH], U32, align_bytes=64)
+        w_s = const.tile([P, FH], U8, align_bytes=64)
+        nc.vector.quantize_mx(
+            out=w_c[:].bitcast(FP8X4), scales=w_s[:], in_=w_grp[:].rearrange("q f t -> q (f t)")
+        )
+
+        a_sb = {}
+        x_sb = {}
+        r_sb = {}
+        r_ps = {}
+        h_c = {}
+        h_s = {}
+
+        def load(g):
+            a_t = apool.tile([P, NB, N], BF16, name="a_sb")
+            src = adj[g].rearrange("(b p) i -> p b i", p=P)
+            nc.sync.dma_start(out=a_t[:, 0:4, :], in_=src[:, 0:4, :])
+            nc.sync.dma_start(out=a_t[:, 4:8, :], in_=src[:, 4:8, :])
+            a_sb[g] = a_t
+            x_t = xpool.tile([P, NB * FI], BF16, name="x_sb")
+            nc.sync.dma_start(
+                out=x_t[:].rearrange("p (b k) -> p b k", b=NB),
+                in_=batch_graph[g].rearrange("(b p) k -> p b k", p=P),
+            )
+            x_sb[g] = x_t
+
+        def xpath(g):
+            x32 = x_sb[g][:].bitcast(F32)
+            xg = xgpool.tile([P, 4 * N], BF16, name="xg", align_bytes=64)
+            xg32 = xg[:].bitcast(F32).rearrange("q (s b n u) -> q s b n u", s=4, b=2, u=2)
+            for s in range(4):
+                xt = ps_xt.tile([P, 2, 2, P], F32, name="xt")
+                for b2 in range(2):
+                    for u in range(2):
+                        col = 256 * (2 * s + b2) + P * u
+                        nc.tensor.transpose(xt[:, b2, u, :], x32[:, col : col + P], ident[:])
+                nc.scalar.copy(out=xg32[:, s], in_=xt[:].rearrange("q b u n -> q b n u"))
+            x_c = xgpool.tile([P, N], U32, name="x_c", align_bytes=64)
+            x_s = xgpool.tile([P, N], U8, name="x_s", align_bytes=64)
+            nc.vector.quantize_mx(out=x_c[:].bitcast(FP8X4), scales=x_s[:], in_=xg[:])
+            hg = hpool.tile([P, 2, FH, 4], BF16, name="hg", align_bytes=64)
+            for c in range(2):
+                h_ps = ps_h.tile([P, 4, FH], F32, name="h_ps")
+                for t in range(4):
+                    cols = slice(P * (4 * c + t), P * (4 * c + t + 1))
+                    nc.tensor.matmul_mx(
+                        out=h_ps[:, t, :],
+                        lhsT=x_c[:, cols].bitcast(FP8X4),
+                        lhsT_scale=x_s[:, cols],
+                        rhs=w_c[:].bitcast(FP8X4),
+                        rhs_scale=w_s[:],
+                        start=True,
+                        stop=True,
+                    )
+                nc.scalar.copy(out=hg[:, c], in_=h_ps[:].rearrange("p t f -> p f t"))
+            hc = hpool.tile([P, 2 * FH], U32, name="hc", align_bytes=64)
+            hs = hpool.tile([P, 2 * FH], U8, name="hs", align_bytes=64)
+            nc.vector.quantize_mx(
+                out=hc[:].bitcast(FP8X4), scales=hs[:], in_=hg[:].rearrange("p c f t -> p (c f t)")
+            )
+            h_c[g] = hc
+            h_s[g] = hs
+
+        def colsum(g):
+            cs = ps_cs.tile([P, NB], F32, name="cs")
+            for ib in range(NB):
+                for b in range(NB):
+                    nc.tensor.matmul(
+                        out=cs[:, ib : ib + 1],
+                        lhsT=a_sb[g][:, b, P * ib : P * (ib + 1)],
+                        rhs=ones[:, 0:1],
+                        start=(b == 0),
+                        stop=(b == NB - 1),
+                    )
+            m1 = small.tile([P, NB], F32, name="m1")
+            nc.vector.tensor_single_scalar(out=m1[:], in_=cs[:], scalar=0.0, op=ALU.is_gt)
+            ns = small.tile([P, NB], F32, name="ns")
+            nc.vector.scalar_tensor_tensor(
+                out=ns[:], in0=m1[:], scalar=1.0, in1=cs[:], op0=ALU.subtract, op1=ALU.subtract
+            )
+            sq = small.tile([P, NB], F32, name="sq")
+            nc.scalar.activation(out=sq[:], in_=ns[:], func=ACT.Sqrt, scale=-1.0)
+            rc = small.tile([P, NB], F32, name="rc")
+            nc.vector.reciprocal(out=rc[:], in_=sq[:])
+            r = small.tile([P, NB], F32, name="r")
+            nc.vector.tensor_tensor(out=r[:], in0=rc[:], in1=m1[:], op=ALU.mult)
+            r_sb[g] = r
+
+        def spread(g, h):
+            rp = ps_r.tile([P, 512], F32, name="rp%d" % h)
+            for k in range(4):
+                nc.tensor.transpose(
+                    rp[:, P * k : P * (k + 1)],
+                    r_sb[g][:, 4 * h + k : 4 * h + k + 1].to_broadcast([P, P]),
+                    ident[:],
+                )
+            r_ps[(g, h)] = rp
+
+        def main(g):
+            codes = {}
+            for c in range(2):
+                t1 = t1pool.tile([P, 4, N], F32, name="t1")
+                for t in range(4):
+                    b = 4 * c + t
+                    if b in A_ON_VECTOR:
+                        nc.vector.tensor_scalar(
+                            out=t1[:, t, :], in0=a_sb[g][:, b, :], scalar1=r_sb[g][:, b : b + 1],
+                            scalar2=None, op0=ALU.mult,
+                        )
+                    else:
+                        nc.scalar.activation(
+                            out=t1[:, t, :], in_=a_sb[g][:, b, :], func=ACT.Copy,
+                            scale=r_sb[g][:, b : b + 1],
+                        )
+                for h in range(2):
+                    ag = agpool.tile([P, 512, 4], BF16, name="ag", align_bytes=64)
+                    nc.vector.tensor_tensor(
+                        out=ag[:],
+                        in0=t1[:, :, 512 * h : 512 * (h + 1)].rearrange("p t i -> p i t"),
+                        in1=r_ps[(g, h)][:].unsqueeze(2).to_broadcast([P, 512, 4]),
+                        op=ALU.mult,
+                    )
+                    if c == 1 and g + 1 < G:
+                        spread(g + 1, h)
+                    a_c = acpool.tile([P, 512], U32, name="a_c", align_bytes=64)
+                    a_s = acpool.tile([P, 512], U8, name="a_s", align_bytes=64)
+                    nc.vector.quantize_mx(
+                        out=a_c[:].bitcast(FP8X4), scales=a_s[:], in_=ag[:].rearrange("p i t -> p (i t)")
+                    )
+                    codes[(c, h)] = (a_c, a_s)
+            for h in range(2):
+                o_ps = ps_o.tile([P, 4, FH], F32, name="o_ps")
+                for k in range(4):
+                    cols = slice(P * k, P * (k + 1))
+                    for c in range(2):
+                        a_c, a_s = codes[(c, h)]
+                        nc.tensor.matmul_mx(
+                            out=o_ps[:, k, :],
+                            lhsT=a_c[:, cols].bitcast(FP8X4),
+                            lhsT_scale=a_s[:, cols],
+                            rhs=h_c[g][:, FH * c : FH * (c + 1)].bitcast(FP8X4),
+                            rhs_scale=h_s[g][:, FH * c : FH * (c + 1)],
+                            start=(c == 0),
+                            stop=(c == 1),
+                        )
+                o_sb = opool.tile([P, 4, FH], F32, name="o_sb")
+                nc.vector.tensor_tensor(
+                    out=o_sb[:], in0=o_ps[:], in1=b_f[:].unsqueeze(1).to_broadcast([P, 4, FH]), op=ALU.add
+                )
+                nc.scalar.activation(out=o_sb[:], in_=o_sb[:], func=ACT.Relu)
+                nc.gpsimd.dma_start(
+                    out=out[g, 512 * h : 512 * (h + 1), :].rearrange("(k p) f -> p k f", p=P), in_=o_sb[:]
+                )
+
+        load(0)
+        load(1)
+        load(2)
+        colsum(0)
+        spread(0, 0)
+        spread(0, 1)
+        xpath(0)
+        for g in range(G):
+            if g + 3 < G:
+                load(g + 3)
+            if g + 1 < G:
+                xpath(g + 1)
+                colsum(g + 1)
+            main(g)

@@ -177,9 +177,9 @@ def tile_gcn_pa_t_kernel(tc, batch_graph, adj, W1, b1, out):
                 for h in range(2):
                     ag = agpool.tile([P, 512, 4], BF16, name="ag", align_bytes=64)
                     nc.vector.tensor_tensor(
-                        out=ag[:],
-                        in0=t1[:, :, 512 * h : 512 * (h + 1)].rearrange("p t i -> p i t"),
-                        in1=r_ps[(g, h)][:].unsqueeze(2).to_broadcast([P, 512, 4]),
+                        out=ag[:].rearrange("p (c i) t -> p c t i", i=4),
+                        in0=t1[:, :, 512 * h : 512 * (h + 1)].rearrange("p t (c i) -> p c t i", i=4),
+                        in1=r_ps[(g, h)][:].rearrange("p (c i) -> p c i", i=4).unsqueeze(2).to_broadcast([P, 128, 4, 4]),
                         op=ALU.mult,
                     )
                     if c == 1 and g + 1 < G:

@@ -17,9 +17,8 @@ N = 1024
 FI = 512
 FH = 128
 NB = N // P
+HALF = 512
 FLOPS = 2 * G * N * FI * FH + 2 * G * N * N * FH
-
-A_ON_VECTOR = (7,)
 
 
 def tile_gcn_pa_t_kernel(tc, batch_graph, adj, W1, b1, out):
@@ -27,28 +26,226 @@ def tile_gcn_pa_t_kernel(tc, batch_graph, adj, W1, b1, out):
     with ExitStack() as ctx:
         const = ctx.enter_context(tc.tile_pool(name="const", bufs=1))
         apool = ctx.enter_context(tc.tile_pool(name="apool", bufs=3))
-        xpool = ctx.enter_context(tc.tile_pool(name="xpool", bufs=3))
+        xpool = ctx.enter_context(tc.tile_pool(name="xpool", bufs=2))
         xgpool = ctx.enter_context(tc.tile_pool(name="xgpool", bufs=2))
         t1pool = ctx.enter_context(tc.tile_pool(name="t1pool", bufs=3))
-        agpool = ctx.enter_context(tc.tile_pool(name="agpool", bufs=4))
+        agpool = ctx.enter_context(tc.tile_pool(name="agpool", bufs=3))
         acpool = ctx.enter_context(tc.tile_pool(name="acpool", bufs=8))
-        hpool = ctx.enter_context(tc.tile_pool(name="hpool", bufs=2))
+        hpool = ctx.enter_context(tc.tile_pool(name="hpool", bufs=3))
         small = ctx.enter_context(tc.tile_pool(name="small", bufs=3))
-        opool = ctx.enter_context(tc.tile_pool(name="opool", bufs=4))
+        opool = ctx.enter_context(tc.tile_pool(name="opool", bufs=3))
         ps_xt = ctx.enter_context(tc.psum_pool(name="ps_xt", bufs=2))
-        ps_h = ctx.enter_context(tc.psum_pool(name="ps_h", bufs=1))
+        ps_ho = ctx.enter_context(tc.psum_pool(name="ps_ho", bufs=3))
         ps_cs = ctx.enter_context(tc.psum_pool(name="ps_cs", bufs=1))
         ps_r = ctx.enter_context(tc.psum_pool(name="ps_r", bufs=1))
-        ps_o = ctx.enter_context(tc.psum_pool(name="ps_o", bufs=2))
+        ctx.enter_context(tc.manual_schedule())
 
-        ident = const.tile([P, P], F32)
-        make_identity(nc, ident[:])
-        ones = const.tile([P, 2], BF16)
-        nc.vector.memset(ones[:], 1.0)
-        warm = const.tile([P, 1], F32)
-        nc.vector.memset(warm[:], 1.0)
-        nc.scalar.activation(out=warm[:], in_=warm[:], func=ACT.Sqrt)
+        a_sb = {}
+        x_sb = {}
+        cs_ps = {}
+        m1_sb = {}
+        ns_sb = {}
+        sq_sb = {}
+        r_sb = {}
+        r_ps = {}
+        xg_sb = {}
+        xt_ps = {}
+        xc_sb = {}
+        hp_ps = {}
+        hg_sb = {}
+        hc_sb = {}
+        t1_sb = {}
+        ag_sb = {}
+        ac_sb = {}
+        o_ps = {}
+        o_sb = {}
 
+        def ok(g):
+            return 0 <= g < G
+
+        def load_a(g):
+            a_t = apool.tile([P, NB, N], BF16, name="a_sb")
+            src = adj[g].rearrange("(b p) i -> p b i", p=P)
+            nc.sync.dma_start(out=a_t[:, 0:4, :], in_=src[:, 0:4, :])
+            nc.sync.dma_start(out=a_t[:, 4:8, :], in_=src[:, 4:8, :])
+            a_sb[g] = a_t
+
+        def load_x(g):
+            x_t = xpool.tile([P, NB * FI], BF16, name="x_sb")
+            nc.sync.dma_start(
+                out=x_t[:].rearrange("p (b k) -> p b k", b=NB),
+                in_=batch_graph[g].rearrange("(b p) k -> p b k", p=P),
+            )
+            x_sb[g] = x_t
+
+        def colsum(g, ib_lo, ib_hi):
+            if ib_lo == 0:
+                cs_ps[g] = ps_cs.tile([P, NB], F32, name="cs")
+            for ib in range(ib_lo, ib_hi):
+                for b in range(NB):
+                    nc.tensor.matmul(
+                        out=cs_ps[g][:, ib : ib + 1],
+                        lhsT=a_sb[g][:, b, P * ib : P * (ib + 1)],
+                        rhs=ones[:, 0:1],
+                        start=(b == 0),
+                        stop=(b == NB - 1),
+                    )
+
+        def chain_a(g):
+            m1 = small.tile([P, NB], F32, name="m1")
+            nc.vector.tensor_single_scalar(out=m1[:], in_=cs_ps[g][:], scalar=0.0, op=ALU.is_gt)
+            ns = small.tile([P, NB], F32, name="ns")
+            nc.vector.scalar_tensor_tensor(
+                out=ns[:], in0=m1[:], scalar=1.0, in1=cs_ps[g][:], op0=ALU.subtract, op1=ALU.subtract
+            )
+            m1_sb[g] = m1
+            ns_sb[g] = ns
+
+        def chain_s(g):
+            sq = small.tile([P, NB], F32, name="sq")
+            nc.scalar.activation(out=sq[:], in_=ns_sb[g][:], func=ACT.Sqrt, scale=-1.0)
+            sq_sb[g] = sq
+
+        def chain_b(g):
+            rc = small.tile([P, NB], F32, name="rc")
+            nc.vector.reciprocal(out=rc[:], in_=sq_sb[g][:])
+            r = small.tile([P, NB], F32, name="r")
+            nc.vector.tensor_tensor(out=r[:], in0=rc[:], in1=m1_sb[g][:], op=ALU.mult)
+            r_sb[g] = r
+
+        def spread(g, h):
+            rp = ps_r.tile([P, HALF], F32, name="rp%d" % h)
+            for k in range(4):
+                nc.tensor.transpose(
+                    rp[:, P * k : P * (k + 1)],
+                    r_sb[g][:, 4 * h + k : 4 * h + k + 1].to_broadcast([P, P]),
+                    ident[:],
+                )
+            r_ps[(g, h)] = rp
+
+        def x_transpose(g, s):
+            x32 = x_sb[g][:].bitcast(F32)
+            xt = ps_xt.tile([P, 2, 2, P], F32, name="xt")
+            for b2 in range(2):
+                for u in range(2):
+                    col = 256 * (2 * s + b2) + P * u
+                    nc.tensor.transpose(xt[:, b2, u, :], x32[:, col : col + P], ident[:])
+            xt_ps[(g, s)] = xt
+
+        def x_copy(g, s):
+            if s == 0:
+                xg_sb[g] = xgpool.tile([P, 4 * N], BF16, name="xg", align_bytes=64)
+            xg32 = xg_sb[g][:].bitcast(F32).rearrange("q (s b n u) -> q s b n u", s=4, b=2, u=2)
+            nc.scalar.copy(out=xg32[:, s], in_=xt_ps[(g, s)][:].rearrange("q b u n -> q b n u"))
+
+        def x_quant(g):
+            x_c = xgpool.tile([P, N], U32, name="x_c", align_bytes=64)
+            x_s = xgpool.tile([P, N], U8, name="x_s", align_bytes=64)
+            nc.vector.quantize_mx(out=x_c[:].bitcast(FP8X4), scales=x_s[:], in_=xg_sb[g][:])
+            xc_sb[g] = (x_c, x_s)
+
+        def h_matmul(g, c):
+            x_c, x_s = xc_sb[g]
+            hp = ps_ho.tile([P, 4, FH], F32, name="ho")
+            for t in range(4):
+                cols = slice(P * (4 * c + t), P * (4 * c + t + 1))
+                nc.tensor.matmul_mx(
+                    out=hp[:, t, :],
+                    lhsT=x_c[:, cols].bitcast(FP8X4),
+                    lhsT_scale=x_s[:, cols],
+                    rhs=w_c[:].bitcast(FP8X4),
+                    rhs_scale=w_s[:],
+                    start=True,
+                    stop=True,
+                )
+            hp_ps[(g, c)] = hp
+
+        def h_copy(g, c):
+            if c == 0:
+                hg_sb[g] = hpool.tile([P, 2, FH, 4], BF16, name="hg", align_bytes=64)
+            nc.scalar.copy(out=hg_sb[g][:, c], in_=hp_ps[(g, c)][:].rearrange("p t f -> p f t"))
+
+        def h_quant(g):
+            hc = hpool.tile([P, 2 * FH], U32, name="hc", align_bytes=64)
+            hs = hpool.tile([P, 2 * FH], U8, name="hs", align_bytes=64)
+            nc.vector.quantize_mx(
+                out=hc[:].bitcast(FP8X4), scales=hs[:], in_=hg_sb[g][:].rearrange("p c f t -> p (c f t)")
+            )
+            hc_sb[g] = (hc, hs)
+
+        def scale_rows(g, b):
+            c = b // 4
+            t = b % 4
+            if t == 0:
+                t1_sb[(g, c)] = t1pool.tile([P, 4, N], F32, name="t1")
+            t1 = t1_sb[(g, c)]
+            if g == 0 and b >= 2:
+                nc.vector.tensor_scalar(
+                    out=t1[:, t, :], in0=a_sb[g][:, b, :], scalar1=r_sb[g][:, b : b + 1],
+                    scalar2=None, op0=ALU.mult,
+                )
+            else:
+                nc.scalar.activation(
+                    out=t1[:, t, :], in_=a_sb[g][:, b, :], func=ACT.Copy, scale=r_sb[g][:, b : b + 1]
+                )
+
+        def scale_cols(g, k):
+            h = k // 2
+            c = k % 2
+            ag = agpool.tile([P, HALF, 4], BF16, name="ag", align_bytes=64)
+            nc.vector.tensor_tensor(
+                out=ag[:].rearrange("p (w i) t -> p w t i", i=4),
+                in0=t1_sb[(g, c)][:, :, HALF * h : HALF * (h + 1)].rearrange("p t (w i) -> p w t i", i=4),
+                in1=r_ps[(g, h)][:].rearrange("p (w i) -> p w i", i=4).unsqueeze(2).to_broadcast([P, P, 4, 4]),
+                op=ALU.mult,
+            )
+            ag_sb[(g, k)] = ag
+
+        def a_quant(g, k):
+            a_c = acpool.tile([P, HALF], U32, name="a_c", align_bytes=64)
+            a_s = acpool.tile([P, HALF], U8, name="a_s", align_bytes=64)
+            nc.vector.quantize_mx(
+                out=a_c[:].bitcast(FP8X4), scales=a_s[:], in_=ag_sb[(g, k)][:].rearrange("p i t -> p (i t)")
+            )
+            ac_sb[(g, k)] = (a_c, a_s)
+
+        def out_matmul(g, h):
+            hc, hs = hc_sb[g]
+            op = ps_ho.tile([P, 4, FH], F32, name="ho")
+            for k in range(4):
+                cols = slice(P * k, P * (k + 1))
+                for c in range(2):
+                    a_c, a_s = ac_sb[(g, 2 * h + c)]
+                    nc.tensor.matmul_mx(
+                        out=op[:, k, :],
+                        lhsT=a_c[:, cols].bitcast(FP8X4),
+                        lhsT_scale=a_s[:, cols],
+                        rhs=hc[:, FH * c : FH * (c + 1)].bitcast(FP8X4),
+                        rhs_scale=hs[:, FH * c : FH * (c + 1)],
+                        start=(c == 0),
+                        stop=(c == 1),
+                    )
+            o_ps[(g, h)] = op
+
+        def out_bias(g, h):
+            o_t = opool.tile([P, 4, FH], F32, name="o_sb")
+            nc.vector.tensor_tensor(
+                out=o_t[:], in0=o_ps[(g, h)][:], in1=b_f[:].unsqueeze(1).to_broadcast([P, 4, FH]), op=ALU.add
+            )
+            o_sb[(g, h)] = o_t
+
+        def out_relu_store(g, h):
+            o_t = o_sb[(g, h)]
+            nc.scalar.activation(out=o_t[:], in_=o_t[:], func=ACT.Relu)
+            nc.gpsimd.dma_start(
+                out=out[g, HALF * h : HALF * (h + 1), :].rearrange("(k p) f -> p k f", p=P), in_=o_t[:]
+            )
+
+        load_a(0)
+        load_x(0)
+        load_a(1)
+        load_x(1)
+        load_a(2)
         w_raw = const.tile([P, 4, FH], BF16)
         nc.scalar.dma_start(
             out=w_raw[:].rearrange("q (u e) f -> q u (e f)", u=2),
@@ -56,6 +253,13 @@ def tile_gcn_pa_t_kernel(tc, batch_graph, adj, W1, b1, out):
         )
         b_bf = const.tile([P, FH], BF16)
         nc.scalar.dma_start(out=b_bf[:], in_=b1.partition_broadcast(P))
+        ident = const.tile([P, P], F32)
+        make_identity(nc, ident[:])
+        ones = const.tile([P, 2], BF16)
+        nc.vector.memset(ones[:], 1.0)
+        warm = const.tile([P, 1], F32)
+        nc.vector.memset(warm[:], 1.0)
+        nc.scalar.activation(out=warm[:], in_=warm[:], func=ACT.Sqrt)
         w_grp = const.tile([P, FH, 4], BF16, align_bytes=64)
         nc.vector.tensor_copy(out=w_grp[:], in_=w_raw[:].rearrange("q t f -> q f t"))
         b_f = const.tile([P, FH], F32)
@@ -66,165 +270,81 @@ def tile_gcn_pa_t_kernel(tc, batch_graph, adj, W1, b1, out):
             out=w_c[:].bitcast(FP8X4), scales=w_s[:], in_=w_grp[:].rearrange("q f t -> q (f t)")
         )
 
-        a_sb = {}
-        x_sb = {}
-        r_sb = {}
-        r_ps = {}
-        h_c = {}
-        h_s = {}
-
-        def load(g):
-            a_t = apool.tile([P, NB, N], BF16, name="a_sb")
-            src = adj[g].rearrange("(b p) i -> p b i", p=P)
-            nc.sync.dma_start(out=a_t[:, 0:4, :], in_=src[:, 0:4, :])
-            nc.sync.dma_start(out=a_t[:, 4:8, :], in_=src[:, 4:8, :])
-            a_sb[g] = a_t
-            x_t = xpool.tile([P, NB * FI], BF16, name="x_sb")
-            nc.sync.dma_start(
-                out=x_t[:].rearrange("p (b k) -> p b k", b=NB),
-                in_=batch_graph[g].rearrange("(b p) k -> p b k", p=P),
-            )
-            x_sb[g] = x_t
-
-        def xpath(g):
-            x32 = x_sb[g][:].bitcast(F32)
-            xg = xgpool.tile([P, 4 * N], BF16, name="xg", align_bytes=64)
-            xg32 = xg[:].bitcast(F32).rearrange("q (s b n u) -> q s b n u", s=4, b=2, u=2)
-            for s in range(4):
-                xt = ps_xt.tile([P, 2, 2, P], F32, name="xt")
-                for b2 in range(2):
-                    for u in range(2):
-                        col = 256 * (2 * s + b2) + P * u
-                        nc.tensor.transpose(xt[:, b2, u, :], x32[:, col : col + P], ident[:])
-                nc.scalar.copy(out=xg32[:, s], in_=xt[:].rearrange("q b u n -> q b n u"))
-            x_c = xgpool.tile([P, N], U32, name="x_c", align_bytes=64)
-            x_s = xgpool.tile([P, N], U8, name="x_s", align_bytes=64)
-            nc.vector.quantize_mx(out=x_c[:].bitcast(FP8X4), scales=x_s[:], in_=xg[:])
-            hg = hpool.tile([P, 2, FH, 4], BF16, name="hg", align_bytes=64)
-            for c in range(2):
-                h_ps = ps_h.tile([P, 4, FH], F32, name="h_ps")
-                for t in range(4):
-                    cols = slice(P * (4 * c + t), P * (4 * c + t + 1))
-                    nc.tensor.matmul_mx(
-                        out=h_ps[:, t, :],
-                        lhsT=x_c[:, cols].bitcast(FP8X4),
-                        lhsT_scale=x_s[:, cols],
-                        rhs=w_c[:].bitcast(FP8X4),
-                        rhs_scale=w_s[:],
-                        start=True,
-                        stop=True,
-                    )
-                nc.scalar.copy(out=hg[:, c], in_=h_ps[:].rearrange("p t f -> p f t"))
-            hc = hpool.tile([P, 2 * FH], U32, name="hc", align_bytes=64)
-            hs = hpool.tile([P, 2 * FH], U8, name="hs", align_bytes=64)
-            nc.vector.quantize_mx(
-                out=hc[:].bitcast(FP8X4), scales=hs[:], in_=hg[:].rearrange("p c f t -> p (c f t)")
-            )
-            h_c[g] = hc
-            h_s[g] = hs
-
-        def colsum(g):
-            cs = ps_cs.tile([P, NB], F32, name="cs")
-            for ib in range(NB):
-                for b in range(NB):
-                    nc.tensor.matmul(
-                        out=cs[:, ib : ib + 1],
-                        lhsT=a_sb[g][:, b, P * ib : P * (ib + 1)],
-                        rhs=ones[:, 0:1],
-                        start=(b == 0),
-                        stop=(b == NB - 1),
-                    )
-            m1 = small.tile([P, NB], F32, name="m1")
-            nc.vector.tensor_single_scalar(out=m1[:], in_=cs[:], scalar=0.0, op=ALU.is_gt)
-            ns = small.tile([P, NB], F32, name="ns")
-            nc.vector.scalar_tensor_tensor(
-                out=ns[:], in0=m1[:], scalar=1.0, in1=cs[:], op0=ALU.subtract, op1=ALU.subtract
-            )
-            sq = small.tile([P, NB], F32, name="sq")
-            nc.scalar.activation(out=sq[:], in_=ns[:], func=ACT.Sqrt, scale=-1.0)
-            rc = small.tile([P, NB], F32, name="rc")
-            nc.vector.reciprocal(out=rc[:], in_=sq[:])
-            r = small.tile([P, NB], F32, name="r")
-            nc.vector.tensor_tensor(out=r[:], in0=rc[:], in1=m1[:], op=ALU.mult)
-            r_sb[g] = r
-
-        def spread(g, h):
-            rp = ps_r.tile([P, 512], F32, name="rp%d" % h)
-            for k in range(4):
-                nc.tensor.transpose(
-                    rp[:, P * k : P * (k + 1)],
-                    r_sb[g][:, 4 * h + k : 4 * h + k + 1].to_broadcast([P, P]),
-                    ident[:],
-                )
-            r_ps[(g, h)] = rp
-
-        def main(g):
-            codes = {}
-            for c in range(2):
-                t1 = t1pool.tile([P, 4, N], F32, name="t1")
-                for t in range(4):
-                    b = 4 * c + t
-                    if b in A_ON_VECTOR:
-                        nc.vector.tensor_scalar(
-                            out=t1[:, t, :], in0=a_sb[g][:, b, :], scalar1=r_sb[g][:, b : b + 1],
-                            scalar2=None, op0=ALU.mult,
-                        )
-                    else:
-                        nc.scalar.activation(
-                            out=t1[:, t, :], in_=a_sb[g][:, b, :], func=ACT.Copy,
-                            scale=r_sb[g][:, b : b + 1],
-                        )
-                for h in range(2):
-                    ag = agpool.tile([P, 512, 4], BF16, name="ag", align_bytes=64)
-                    nc.vector.tensor_tensor(
-                        out=ag[:].rearrange("p (c i) t -> p c t i", i=4),
-                        in0=t1[:, :, 512 * h : 512 * (h + 1)].rearrange("p t (c i) -> p c t i", i=4),
-                        in1=r_ps[(g, h)][:].rearrange("p (c i) -> p c i", i=4).unsqueeze(2).to_broadcast([P, 128, 4, 4]),
-                        op=ALU.mult,
-                    )
-                    if c == 1 and g + 1 < G:
-                        spread(g + 1, h)
-                    a_c = acpool.tile([P, 512], U32, name="a_c", align_bytes=64)
-                    a_s = acpool.tile([P, 512], U8, name="a_s", align_bytes=64)
-                    nc.vector.quantize_mx(
-                        out=a_c[:].bitcast(FP8X4), scales=a_s[:], in_=ag[:].rearrange("p i t -> p (i t)")
-                    )
-                    codes[(c, h)] = (a_c, a_s)
-            for h in range(2):
-                o_ps = ps_o.tile([P, 4, FH], F32, name="o_ps")
-                for k in range(4):
-                    cols = slice(P * k, P * (k + 1))
-                    for c in range(2):
-                        a_c, a_s = codes[(c, h)]
-                        nc.tensor.matmul_mx(
-                            out=o_ps[:, k, :],
-                            lhsT=a_c[:, cols].bitcast(FP8X4),
-                            lhsT_scale=a_s[:, cols],
-                            rhs=h_c[g][:, FH * c : FH * (c + 1)].bitcast(FP8X4),
-                            rhs_scale=h_s[g][:, FH * c : FH * (c + 1)],
-                            start=(c == 0),
-                            stop=(c == 1),
-                        )
-                o_sb = opool.tile([P, 4, FH], F32, name="o_sb")
-                nc.vector.tensor_tensor(
-                    out=o_sb[:], in0=o_ps[:], in1=b_f[:].unsqueeze(1).to_broadcast([P, 4, FH]), op=ALU.add
-                )
-                nc.scalar.activation(out=o_sb[:], in_=o_sb[:], func=ACT.Relu)
-                nc.gpsimd.dma_start(
-                    out=out[g, 512 * h : 512 * (h + 1), :].rearrange("(k p) f -> p k f", p=P), in_=o_sb[:]
-                )
-
-        load(0)
-        load(1)
-        load(2)
-        colsum(0)
+        colsum(0, 0, NB)
+        chain_a(0)
+        chain_s(0)
+        chain_b(0)
         spread(0, 0)
         spread(0, 1)
-        xpath(0)
-        for g in range(G):
-            if g + 3 < G:
-                load(g + 3)
-            if g + 1 < G:
-                xpath(g + 1)
-                colsum(g + 1)
-            main(g)
+
+        for g in range(-1, G + 1):
+            if ok(g) and g >= 1:
+                spread(g, 1)
+            if ok(g + 2):
+                colsum(g + 2, 0, 4)
+            if ok(g):
+                scale_rows(g, 6)
+                scale_rows(g, 7)
+                scale_cols(g, 0)
+            if ok(g + 1) and g >= 0:
+                chain_a(g + 1)
+                chain_s(g + 1)
+            if ok(g - 1):
+                a_quant(g - 1, 3)
+                out_bias(g - 1, 0)
+            if ok(g):
+                x_quant(g)
+            if ok(g + 1) and g >= 0:
+                chain_b(g + 1)
+            if ok(g + 3) and g >= 0:
+                load_x(g + 2) if ok(g + 2) else None
+                load_a(g + 3)
+            elif ok(g + 2) and g >= 0:
+                load_x(g + 2)
+            if ok(g - 1):
+                out_matmul(g - 1, 1)
+            if ok(g):
+                h_matmul(g, 0)
+                h_matmul(g, 1)
+            if ok(g + 2):
+                colsum(g + 2, 4, NB)
+            if ok(g + 1):
+                scale_rows(g + 1, 0)
+                scale_rows(g + 1, 1)
+            if ok(g):
+                h_copy(g, 0)
+                h_copy(g, 1)
+            if ok(g - 1):
+                out_relu_store(g - 1, 0)
+            if ok(g):
+                scale_cols(g, 1)
+                a_quant(g, 0)
+            if ok(g + 1) and g >= 0:
+                spread(g + 1, 0)
+            if ok(g + 1):
+                x_transpose(g + 1, 0)
+                x_transpose(g + 1, 1)
+                scale_rows(g + 1, 2)
+                scale_rows(g + 1, 3)
+                x_copy(g + 1, 0)
+                x_copy(g + 1, 1)
+            if ok(g):
+                scale_cols(g, 2)
+                a_quant(g, 1)
+                h_quant(g)
+            if ok(g - 1):
+                out_bias(g - 1, 1)
+            if ok(g):
+                out_matmul(g, 0)
+            if ok(g + 1):
+                x_transpose(g + 1, 2)
+                x_transpose(g + 1, 3)
+                scale_rows(g + 1, 4)
+                scale_rows(g + 1, 5)
+                x_copy(g + 1, 2)
+                x_copy(g + 1, 3)
+            if ok(g - 1):
+                out_relu_store(g - 1, 1)
+            if ok(g):
+                scale_cols(g, 3)
+                a_quant(g, 2)

@@ -18,6 +18,8 @@ FI = 512
 FH = 128
 NB = N // P
 HALF = 512
+XG = 128
+XV = HALF - XG
 FLOPS = 2 * G * N * FI * FH + 2 * G * N * N * FH
 
 
@@ -29,7 +31,7 @@ def tile_gcn_pa_t_kernel(tc, batch_graph, adj, W1, b1, out):
         xpool = ctx.enter_context(tc.tile_pool(name="xpool", bufs=2))
         xgpool = ctx.enter_context(tc.tile_pool(name="xgpool", bufs=2))
         t1pool = ctx.enter_context(tc.tile_pool(name="t1pool", bufs=3))
-        agpool = ctx.enter_context(tc.tile_pool(name="agpool", bufs=3))
+        agpool = ctx.enter_context(tc.tile_pool(name="agpool", bufs=2))
         acpool = ctx.enter_context(tc.tile_pool(name="acpool", bufs=8))
         hpool = ctx.enter_context(tc.tile_pool(name="hpool", bufs=3))
         small = ctx.enter_context(tc.tile_pool(name="small", bufs=3))
@@ -48,6 +50,7 @@ def tile_gcn_pa_t_kernel(tc, batch_graph, adj, W1, b1, out):
         sq_sb = {}
         r_sb = {}
         r_ps = {}
+        rg_sb = {}
         xg_sb = {}
         xt_ps = {}
         xc_sb = {}
@@ -123,6 +126,11 @@ def tile_gcn_pa_t_kernel(tc, batch_graph, adj, W1, b1, out):
                 )
             r_ps[(g, h)] = rp
 
+        def spread_copy(g, h):
+            rg = small.tile([P, XG], F32, name="rg%d" % h)
+            nc.scalar.copy(out=rg[:], in_=r_ps[(g, h)][:, XV:HALF])
+            rg_sb[(g, h)] = rg
+
         def x_transpose(g, s):
             x32 = x_sb[g][:].bitcast(F32)
             xt = ps_xt.tile([P, 2, 2, P], F32, name="xt")
@@ -193,10 +201,23 @@ def tile_gcn_pa_t_kernel(tc, batch_graph, adj, W1, b1, out):
             h = k // 2
             c = k % 2
             ag = agpool.tile([P, HALF, 4], BF16, name="ag", align_bytes=64)
+            lo = HALF * h
             nc.vector.tensor_tensor(
-                out=ag[:].rearrange("p (w i) t -> p w t i", i=4),
-                in0=t1_sb[(g, c)][:, :, HALF * h : HALF * (h + 1)].rearrange("p t (w i) -> p w t i", i=4),
-                in1=r_ps[(g, h)][:].rearrange("p (w i) -> p w i", i=4).unsqueeze(2).to_broadcast([P, P, 4, 4]),
+                out=ag[:, 0:XV, :].rearrange("p (w i) t -> p w t i", i=4),
+                in0=t1_sb[(g, c)][:, :, lo : lo + XV].rearrange("p t (w i) -> p w t i", i=4),
+                in1=r_ps[(g, h)][:, 0:XV]
+                .rearrange("p (w i) -> p w i", i=4)
+                .unsqueeze(2)
+                .to_broadcast([P, XV // 4, 4, 4]),
+                op=ALU.mult,
+            )
+            nc.gpsimd.tensor_tensor(
+                out=ag[:, XV:HALF, :].rearrange("p (w i) t -> p w t i", i=4),
+                in0=t1_sb[(g, c)][:, :, lo + XV : lo + HALF].rearrange("p t (w i) -> p w t i", i=4),
+                in1=rg_sb[(g, h)][:]
+                .rearrange("p (w i) -> p w i", i=4)
+                .unsqueeze(2)
+                .to_broadcast([P, XG // 4, 4, 4]),
                 op=ALU.mult,
             )
             ag_sb[(g, k)] = ag
@@ -237,7 +258,7 @@ def tile_gcn_pa_t_kernel(tc, batch_graph, adj, W1, b1, out):
         def out_relu_store(g, h):
             o_t = o_sb[(g, h)]
             nc.scalar.activation(out=o_t[:], in_=o_t[:], func=ACT.Relu)
-            nc.gpsimd.dma_start(
+            nc.sync.dma_start(
                 out=out[g, HALF * h : HALF * (h + 1), :].rearrange("(k p) f -> p k f", p=P), in_=o_t[:]
             )
 
@@ -276,6 +297,8 @@ def tile_gcn_pa_t_kernel(tc, batch_graph, adj, W1, b1, out):
         chain_b(0)
         spread(0, 0)
         spread(0, 1)
+        spread_copy(0, 0)
+        spread_copy(0, 1)
 
         for g in range(-1, G + 1):
             if ok(g) and g >= 1:
@@ -285,17 +308,20 @@ def tile_gcn_pa_t_kernel(tc, batch_graph, adj, W1, b1, out):
             if ok(g):
                 scale_rows(g, 6)
                 scale_rows(g, 7)
+                if g >= 1:
+                    spread_copy(g, 1)
                 scale_cols(g, 0)
             if ok(g + 1) and g >= 0:
                 chain_a(g + 1)
                 chain_s(g + 1)
             if ok(g - 1):
-                a_quant(g - 1, 3)
                 out_bias(g - 1, 0)
             if ok(g):
                 x_quant(g)
             if ok(g + 1) and g >= 0:
                 chain_b(g + 1)
+            if ok(g - 1):
+                a_quant(g - 1, 3)
             if ok(g + 3) and g >= 0:
                 load_x(g + 2) if ok(g + 2) else None
                 load_a(g + 3)
@@ -330,10 +356,11 @@ def tile_gcn_pa_t_kernel(tc, batch_graph, adj, W1, b1, out):
                 x_copy(g + 1, 1)
             if ok(g):
                 scale_cols(g, 2)
-                a_quant(g, 1)
                 h_quant(g)
             if ok(g - 1):
                 out_bias(g - 1, 1)
+            if ok(g):
+                a_quant(g, 1)
             if ok(g):
                 out_matmul(g, 0)
             if ok(g + 1):
@@ -343,6 +370,8 @@ def tile_gcn_pa_t_kernel(tc, batch_graph, adj, W1, b1, out):
                 scale_rows(g + 1, 5)
                 x_copy(g + 1, 2)
                 x_copy(g + 1, 3)
+                if g >= 0:
+                    spread_copy(g + 1, 0)
             if ok(g - 1):
                 out_relu_store(g - 1, 1)
             if ok(g):

@@ -212,12 +212,9 @@ def tile_gcn_pa_t_kernel(tc, batch_graph, adj, W1, b1, out):
                 op=ALU.mult,
             )
             nc.gpsimd.tensor_tensor(
-                out=ag[:, XV:HALF, :].rearrange("p (w i) t -> p w t i", i=4),
-                in0=t1_sb[(g, c)][:, :, lo + XV : lo + HALF].rearrange("p t (w i) -> p w t i", i=4),
-                in1=rg_sb[(g, h)][:]
-                .rearrange("p (w i) -> p w i", i=4)
-                .unsqueeze(2)
-                .to_broadcast([P, XG // 4, 4, 4]),
+                out=ag[:, XV:HALF, :],
+                in0=t1_sb[(g, c)][:, :, lo + XV : lo + HALF].rearrange("p t i -> p i t"),
+                in1=rg_sb[(g, h)][:].unsqueeze(2).to_broadcast([P, XG, 4]),
                 op=ALU.mult,
             )
             ag_sb[(g, k)] = ag

@@ -18,7 +18,7 @@ FI = 512
 FH = 128
 NB = N // P
 HALF = 512
-XG = 128
+XG = 160
 XV = HALF - XG
 FLOPS = 2 * G * N * FI * FH + 2 * G * N * N * FH
 
@@ -187,7 +187,7 @@ def tile_gcn_pa_t_kernel(tc, batch_graph, adj, W1, b1, out):
             if t == 0:
                 t1_sb[(g, c)] = t1pool.tile([P, 4, N], F32, name="t1")
             t1 = t1_sb[(g, c)]
-            if g == 0 and b >= 2:
+            if b % 4 == 3 or (g == 0 and b % 2 == 1):
                 nc.vector.tensor_scalar(
                     out=t1[:, t, :], in0=a_sb[g][:, b, :], scalar1=r_sb[g][:, b : b + 1],
                     scalar2=None, op0=ALU.mult,
@@ -259,8 +259,8 @@ def tile_gcn_pa_t_kernel(tc, batch_graph, adj, W1, b1, out):
                 out=out[g, HALF * h : HALF * (h + 1), :].rearrange("(k p) f -> p k f", p=P), in_=o_t[:]
             )
 
-        load_a(0)
         load_x(0)
+        load_a(0)
         load_a(1)
         load_x(1)
         load_a(2)
@@ -288,69 +288,82 @@ def tile_gcn_pa_t_kernel(tc, batch_graph, adj, W1, b1, out):
             out=w_c[:].bitcast(FP8X4), scales=w_s[:], in_=w_grp[:].rearrange("q f t -> q (f t)")
         )
 
+        for s in range(4):
+            x_transpose(0, s)
+            x_copy(0, s)
+        x_quant(0)
         colsum(0, 0, NB)
         chain_a(0)
         chain_s(0)
         chain_b(0)
         spread(0, 0)
         spread(0, 1)
+        for b in range(NB):
+            scale_rows(0, b)
         spread_copy(0, 0)
         spread_copy(0, 1)
 
+        def later(g):
+            return 1 <= g < G
+
         for g in range(-1, G + 1):
-            if ok(g) and g >= 1:
-                spread(g, 1)
-            if ok(g + 2):
-                colsum(g + 2, 0, 4)
-            if ok(g):
-                scale_rows(g, 6)
-                scale_rows(g, 7)
-                if g >= 1:
-                    spread_copy(g, 1)
-                scale_cols(g, 0)
-            if ok(g + 1) and g >= 0:
-                chain_a(g + 1)
-                chain_s(g + 1)
-            if ok(g - 1):
-                out_bias(g - 1, 0)
-            if ok(g):
-                x_quant(g)
-            if ok(g + 1) and g >= 0:
-                chain_b(g + 1)
-            if ok(g - 1):
-                a_quant(g - 1, 3)
-            if ok(g + 3) and g >= 0:
-                load_x(g + 2) if ok(g + 2) else None
-                load_a(g + 3)
-            elif ok(g + 2) and g >= 0:
-                load_x(g + 2)
-            if ok(g - 1):
-                out_matmul(g - 1, 1)
             if ok(g):
                 h_matmul(g, 0)
                 h_matmul(g, 1)
+            if later(g):
+                spread(g, 1)
+            if later(g + 1):
+                x_transpose(g + 1, 0)
+                x_transpose(g + 1, 1)
+            if ok(g + 2):
+                colsum(g + 2, 0, 4)
+            if later(g):
+                scale_rows(g, 6)
+            if ok(g):
+                scale_cols(g, 0)
+            if later(g + 1):
+                chain_a(g + 1)
+                chain_s(g + 1)
+                x_copy(g + 1, 0)
+                x_copy(g + 1, 1)
+            if later(g):
+                spread_copy(g, 1)
+            if ok(g - 1):
+                out_bias(g - 1, 0)
+            if later(g):
+                scale_rows(g, 7)
+            if later(g + 1):
+                chain_b(g + 1)
+            if ok(g - 1):
+                a_quant(g - 1, 3)
+            if g >= 0 and ok(g + 2):
+                load_x(g + 2)
+            if g >= 0 and ok(g + 3):
+                load_a(g + 3)
+            if ok(g - 1):
+                out_matmul(g - 1, 1)
             if ok(g + 2):
                 colsum(g + 2, 4, NB)
-            if ok(g + 1):
+            if later(g + 1):
                 scale_rows(g + 1, 0)
                 scale_rows(g + 1, 1)
             if ok(g):
                 h_copy(g, 0)
                 h_copy(g, 1)
+                scale_cols(g, 1)
+            if later(g + 1):
+                scale_rows(g + 1, 3)
+            if ok(g):
+                a_quant(g, 0)
+            if later(g + 1):
+                spread(g + 1, 0)
+                x_transpose(g + 1, 2)
+                x_transpose(g + 1, 3)
+                scale_rows(g + 1, 2)
+                x_copy(g + 1, 2)
+                x_copy(g + 1, 3)
             if ok(g - 1):
                 out_relu_store(g - 1, 0)
-            if ok(g):
-                scale_cols(g, 1)
-                a_quant(g, 0)
-            if ok(g + 1) and g >= 0:
-                spread(g + 1, 0)
-            if ok(g + 1):
-                x_transpose(g + 1, 0)
-                x_transpose(g + 1, 1)
-                scale_rows(g + 1, 2)
-                scale_rows(g + 1, 3)
-                x_copy(g + 1, 0)
-                x_copy(g + 1, 1)
             if ok(g):
                 scale_cols(g, 2)
                 h_quant(g)
@@ -360,17 +373,15 @@ def tile_gcn_pa_t_kernel(tc, batch_graph, adj, W1, b1, out):
                 a_quant(g, 1)
             if ok(g):
                 out_matmul(g, 0)
-            if ok(g + 1):
-                x_transpose(g + 1, 2)
-                x_transpose(g + 1, 3)
+            if later(g + 1):
                 scale_rows(g + 1, 4)
                 scale_rows(g + 1, 5)
-                x_copy(g + 1, 2)
-                x_copy(g + 1, 3)
-                if g >= 0:
-                    spread_copy(g + 1, 0)
+                spread_copy(g + 1, 0)
             if ok(g - 1):
                 out_relu_store(g - 1, 1)
             if ok(g):
                 scale_cols(g, 3)
+            if later(g + 1):
+                x_quant(g + 1)
+            if ok(g):
                 a_quant(g, 2)

@@ -12,376 +12,365 @@ ALU = mybir.AluOpType
 ACT = mybir.ActivationFunctionType
 
 P = 128
-G = 8
-N = 1024
-FI = 512
-FH = 128
-NB = N // P
+PACK = 4
+GRAPHS = 8
+NODES = 1024
+F_IN = 512
+F_HID = 128
+ROW_TILES = NODES // P
 HALF = 512
-XG = 160
-XV = HALF - XG
-FLOPS = 2 * G * N * FI * FH + 2 * G * N * N * FH
+GPSIMD_COLS = 128
+VECTOR_COLS = HALF - GPSIMD_COLS
+VECTOR_ROW_TILE = 7
+FLOPS = 2 * GRAPHS * NODES * F_IN * F_HID + 2 * GRAPHS * NODES * NODES * F_HID
 
 
 def tile_gcn_pa_t_kernel(tc, batch_graph, adj, W1, b1, out):
     nc = tc.nc
     with ExitStack() as ctx:
         const = ctx.enter_context(tc.tile_pool(name="const", bufs=1))
-        apool = ctx.enter_context(tc.tile_pool(name="apool", bufs=3))
-        xpool = ctx.enter_context(tc.tile_pool(name="xpool", bufs=2))
-        xgpool = ctx.enter_context(tc.tile_pool(name="xgpool", bufs=2))
-        t1pool = ctx.enter_context(tc.tile_pool(name="t1pool", bufs=3))
-        agpool = ctx.enter_context(tc.tile_pool(name="agpool", bufs=2))
-        acpool = ctx.enter_context(tc.tile_pool(name="acpool", bufs=8))
-        hpool = ctx.enter_context(tc.tile_pool(name="hpool", bufs=3))
+        adj_pool = ctx.enter_context(tc.tile_pool(name="adj_pool", bufs=3))
+        x_pool = ctx.enter_context(tc.tile_pool(name="x_pool", bufs=2))
+        xq_pool = ctx.enter_context(tc.tile_pool(name="xq_pool", bufs=2))
+        rows_pool = ctx.enter_context(tc.tile_pool(name="rows_pool", bufs=3))
+        unit_pool = ctx.enter_context(tc.tile_pool(name="unit_pool", bufs=2))
+        aq_pool = ctx.enter_context(tc.tile_pool(name="aq_pool", bufs=8))
+        h_pool = ctx.enter_context(tc.tile_pool(name="h_pool", bufs=3))
         small = ctx.enter_context(tc.tile_pool(name="small", bufs=3))
-        opool = ctx.enter_context(tc.tile_pool(name="opool", bufs=3))
-        ps_xt = ctx.enter_context(tc.psum_pool(name="ps_xt", bufs=2))
-        ps_ho = ctx.enter_context(tc.psum_pool(name="ps_ho", bufs=3))
-        ps_cs = ctx.enter_context(tc.psum_pool(name="ps_cs", bufs=1))
-        ps_r = ctx.enter_context(tc.psum_pool(name="ps_r", bufs=1))
+        out_pool = ctx.enter_context(tc.tile_pool(name="out_pool", bufs=3))
+        psum_x = ctx.enter_context(tc.psum_pool(name="psum_x", bufs=2))
+        psum_mx = ctx.enter_context(tc.psum_pool(name="psum_mx", bufs=3))
+        psum_sum = ctx.enter_context(tc.psum_pool(name="psum_sum", bufs=1))
+        psum_r = ctx.enter_context(tc.psum_pool(name="psum_r", bufs=1))
         ctx.enter_context(tc.manual_schedule())
 
-        a_sb = {}
-        x_sb = {}
-        cs_ps = {}
-        m1_sb = {}
-        ns_sb = {}
-        sq_sb = {}
-        r_sb = {}
-        r_ps = {}
-        rg_sb = {}
-        xg_sb = {}
-        xt_ps = {}
-        xc_sb = {}
-        hp_ps = {}
-        hg_sb = {}
-        hc_sb = {}
-        t1_sb = {}
-        ag_sb = {}
-        ac_sb = {}
-        o_ps = {}
-        o_sb = {}
+        live = {}
 
-        def ok(g):
-            return 0 <= g < G
-
-        def load_a(g):
-            a_t = apool.tile([P, NB, N], BF16, name="a_sb")
-            src = adj[g].rearrange("(b p) i -> p b i", p=P)
-            nc.sync.dma_start(out=a_t[:, 0:4, :], in_=src[:, 0:4, :])
-            nc.sync.dma_start(out=a_t[:, 4:8, :], in_=src[:, 4:8, :])
-            a_sb[g] = a_t
+        def load_adj(g):
+            tile = adj_pool.tile([P, ROW_TILES, NODES], BF16, name="adj_sb")
+            rows = adj[g].rearrange("(b p) i -> p b i", p=P)
+            for c in range(2):
+                nc.sync.dma_start(out=tile[:, 4 * c : 4 * c + 4, :], in_=rows[:, 4 * c : 4 * c + 4, :])
+            live["adj", g] = tile
 
         def load_x(g):
-            x_t = xpool.tile([P, NB * FI], BF16, name="x_sb")
+            tile = x_pool.tile([P, ROW_TILES * F_IN], BF16, name="x_sb")
             nc.sync.dma_start(
-                out=x_t[:].rearrange("p (b k) -> p b k", b=NB),
+                out=tile[:].rearrange("p (b k) -> p b k", b=ROW_TILES),
                 in_=batch_graph[g].rearrange("(b p) k -> p b k", p=P),
             )
-            x_sb[g] = x_t
+            live["x", g] = tile
 
-        def colsum(g, ib_lo, ib_hi):
-            if ib_lo == 0:
-                cs_ps[g] = ps_cs.tile([P, NB], F32, name="cs")
-            for ib in range(ib_lo, ib_hi):
-                for b in range(NB):
-                    nc.tensor.matmul(
-                        out=cs_ps[g][:, ib : ib + 1],
-                        lhsT=a_sb[g][:, b, P * ib : P * (ib + 1)],
-                        rhs=ones[:, 0:1],
-                        start=(b == 0),
-                        stop=(b == NB - 1),
-                    )
-
-        def chain_a(g):
-            m1 = small.tile([P, NB], F32, name="m1")
-            nc.vector.tensor_single_scalar(out=m1[:], in_=cs_ps[g][:], scalar=0.0, op=ALU.is_gt)
-            ns = small.tile([P, NB], F32, name="ns")
-            nc.vector.scalar_tensor_tensor(
-                out=ns[:], in0=m1[:], scalar=1.0, in1=cs_ps[g][:], op0=ALU.subtract, op1=ALU.subtract
-            )
-            m1_sb[g] = m1
-            ns_sb[g] = ns
-
-        def chain_s(g):
-            sq = small.tile([P, NB], F32, name="sq")
-            nc.scalar.activation(out=sq[:], in_=ns_sb[g][:], func=ACT.Sqrt, scale=-1.0)
-            sq_sb[g] = sq
-
-        def chain_b(g):
-            rc = small.tile([P, NB], F32, name="rc")
-            nc.vector.reciprocal(out=rc[:], in_=sq_sb[g][:])
-            r = small.tile([P, NB], F32, name="r")
-            nc.vector.tensor_tensor(out=r[:], in0=rc[:], in1=m1_sb[g][:], op=ALU.mult)
-            r_sb[g] = r
-
-        def spread(g, h):
-            rp = ps_r.tile([P, HALF], F32, name="rp%d" % h)
-            for k in range(4):
-                nc.tensor.transpose(
-                    rp[:, P * k : P * (k + 1)],
-                    r_sb[g][:, 4 * h + k : 4 * h + k + 1].to_broadcast([P, P]),
-                    ident[:],
-                )
-            r_ps[(g, h)] = rp
-
-        def spread_copy(g, h):
-            rg = small.tile([P, XG], F32, name="rg%d" % h)
-            nc.scalar.copy(out=rg[:], in_=r_ps[(g, h)][:, XV:HALF])
-            rg_sb[(g, h)] = rg
-
-        def x_transpose(g, s):
-            x32 = x_sb[g][:].bitcast(F32)
-            xt = ps_xt.tile([P, 2, 2, P], F32, name="xt")
+        def transpose_x(g, s):
+            words = live["x", g][:].bitcast(F32)
+            bank = psum_x.tile([P, 2, 2, P], F32, name="xT_ps")
             for b2 in range(2):
                 for u in range(2):
-                    col = 256 * (2 * s + b2) + P * u
-                    nc.tensor.transpose(xt[:, b2, u, :], x32[:, col : col + P], ident[:])
-            xt_ps[(g, s)] = xt
+                    first = (F_IN // 2) * (2 * s + b2) + P * u
+                    nc.tensor.transpose(bank[:, b2, u, :], words[:, first : first + P], ident[:])
+            live["xT", g, s] = bank
 
-        def x_copy(g, s):
+        def copy_x(g, s):
             if s == 0:
-                xg_sb[g] = xgpool.tile([P, 4 * N], BF16, name="xg", align_bytes=64)
-            xg32 = xg_sb[g][:].bitcast(F32).rearrange("q (s b n u) -> q s b n u", s=4, b=2, u=2)
-            nc.scalar.copy(out=xg32[:, s], in_=xt_ps[(g, s)][:].rearrange("q b u n -> q b n u"))
+                live["xg", g] = xq_pool.tile([P, PACK * NODES], BF16, name="x_grouped", align_bytes=64)
+            grouped = live["xg", g][:].bitcast(F32).rearrange("q (s b n u) -> q s b n u", s=4, b=2, u=2)
+            nc.scalar.copy(out=grouped[:, s], in_=live["xT", g, s][:].rearrange("q b u n -> q b n u"))
 
-        def x_quant(g):
-            x_c = xgpool.tile([P, N], U32, name="x_c", align_bytes=64)
-            x_s = xgpool.tile([P, N], U8, name="x_s", align_bytes=64)
-            nc.vector.quantize_mx(out=x_c[:].bitcast(FP8X4), scales=x_s[:], in_=xg_sb[g][:])
-            xc_sb[g] = (x_c, x_s)
+        def quantise_x(g):
+            codes = xq_pool.tile([P, NODES], U32, name="x_codes", align_bytes=64)
+            scales = xq_pool.tile([P, NODES], U8, name="x_scales", align_bytes=64)
+            nc.vector.quantize_mx(out=codes[:].bitcast(FP8X4), scales=scales[:], in_=live["xg", g][:])
+            live["xq", g] = (codes, scales)
 
-        def h_matmul(g, c):
-            x_c, x_s = xc_sb[g]
-            hp = ps_ho.tile([P, 4, FH], F32, name="ho")
-            for t in range(4):
-                cols = slice(P * (4 * c + t), P * (4 * c + t + 1))
+        def matmul_h(g, c):
+            codes, scales = live["xq", g]
+            bank = psum_mx.tile([P, PACK, F_HID], F32, name="mx_ps")
+            for t in range(PACK):
+                nodes = slice(P * (PACK * c + t), P * (PACK * c + t + 1))
                 nc.tensor.matmul_mx(
-                    out=hp[:, t, :],
-                    lhsT=x_c[:, cols].bitcast(FP8X4),
-                    lhsT_scale=x_s[:, cols],
-                    rhs=w_c[:].bitcast(FP8X4),
-                    rhs_scale=w_s[:],
+                    out=bank[:, t, :],
+                    lhsT=codes[:, nodes].bitcast(FP8X4),
+                    lhsT_scale=scales[:, nodes],
+                    rhs=w_codes[:].bitcast(FP8X4),
+                    rhs_scale=w_scales[:],
                     start=True,
                     stop=True,
                 )
-            hp_ps[(g, c)] = hp
+            live["h_ps", g, c] = bank
 
-        def h_copy(g, c):
+        def copy_h(g, c):
             if c == 0:
-                hg_sb[g] = hpool.tile([P, 2, FH, 4], BF16, name="hg", align_bytes=64)
-            nc.scalar.copy(out=hg_sb[g][:, c], in_=hp_ps[(g, c)][:].rearrange("p t f -> p f t"))
+                live["hg", g] = h_pool.tile([P, 2, F_HID, PACK], BF16, name="h_grouped", align_bytes=64)
+            nc.scalar.copy(out=live["hg", g][:, c], in_=live["h_ps", g, c][:].rearrange("p t f -> p f t"))
 
-        def h_quant(g):
-            hc = hpool.tile([P, 2 * FH], U32, name="hc", align_bytes=64)
-            hs = hpool.tile([P, 2 * FH], U8, name="hs", align_bytes=64)
+        def quantise_h(g):
+            codes = h_pool.tile([P, 2 * F_HID], U32, name="h_codes", align_bytes=64)
+            scales = h_pool.tile([P, 2 * F_HID], U8, name="h_scales", align_bytes=64)
             nc.vector.quantize_mx(
-                out=hc[:].bitcast(FP8X4), scales=hs[:], in_=hg_sb[g][:].rearrange("p c f t -> p (c f t)")
+                out=codes[:].bitcast(FP8X4),
+                scales=scales[:],
+                in_=live["hg", g][:].rearrange("p c f t -> p (c f t)"),
             )
-            hc_sb[g] = (hc, hs)
+            live["hq", g] = (codes, scales)
+
+        def column_sums(g, first, last):
+            if first == 0:
+                live["sum", g] = psum_sum.tile([P, ROW_TILES], F32, name="sum_ps")
+            for b in range(first, last):
+                for rows in range(ROW_TILES):
+                    nc.tensor.matmul(
+                        out=live["sum", g][:, b : b + 1],
+                        lhsT=live["adj", g][:, rows, P * b : P * (b + 1)],
+                        rhs=ones[:],
+                        start=(rows == 0),
+                        stop=(rows == ROW_TILES - 1),
+                    )
+
+        def inv_sqrt_start(g):
+            positive = small.tile([P, ROW_TILES], F32, name="positive")
+            nc.vector.tensor_single_scalar(out=positive[:], in_=live["sum", g][:], scalar=0.0, op=ALU.is_gt)
+            minus_safe = small.tile([P, ROW_TILES], F32, name="minus_safe")
+            nc.vector.scalar_tensor_tensor(
+                out=minus_safe[:],
+                in0=positive[:],
+                scalar=1.0,
+                in1=live["sum", g][:],
+                op0=ALU.subtract,
+                op1=ALU.subtract,
+            )
+            live["positive", g] = positive
+            live["minus_safe", g] = minus_safe
+
+        def inv_sqrt_root(g):
+            root = small.tile([P, ROW_TILES], F32, name="root")
+            nc.scalar.activation(out=root[:], in_=live["minus_safe", g][:], func=ACT.Sqrt, scale=-1.0)
+            live["root", g] = root
+
+        def inv_sqrt_finish(g):
+            inverse = small.tile([P, ROW_TILES], F32, name="inverse")
+            nc.vector.reciprocal(out=inverse[:], in_=live["root", g][:])
+            r = small.tile([P, ROW_TILES], F32, name="r")
+            nc.vector.tensor_tensor(out=r[:], in0=inverse[:], in1=live["positive", g][:], op=ALU.mult)
+            live["r", g] = r
+
+        def spread_r(g, h):
+            bank = psum_r.tile([P, HALF], F32, name="r_ps%d" % h)
+            for t in range(PACK):
+                b = PACK * h + t
+                nc.tensor.transpose(
+                    bank[:, P * t : P * (t + 1)], live["r", g][:, b : b + 1].to_broadcast([P, P]), ident[:]
+                )
+            live["r_ps", g, h] = bank
+
+        def copy_spread_r(g, h):
+            tile = small.tile([P, GPSIMD_COLS], F32, name="r_sb%d" % h)
+            nc.scalar.copy(out=tile[:], in_=live["r_ps", g, h][:, VECTOR_COLS:HALF])
+            live["r_sb", g, h] = tile
 
         def scale_rows(g, b):
-            c = b // 4
-            t = b % 4
+            c = b // PACK
+            t = b % PACK
             if t == 0:
-                t1_sb[(g, c)] = t1pool.tile([P, 4, N], F32, name="t1")
-            t1 = t1_sb[(g, c)]
-            if b % 4 == 3 or (g == 0 and b % 2 == 1):
-                nc.vector.tensor_scalar(
-                    out=t1[:, t, :], in0=a_sb[g][:, b, :], scalar1=r_sb[g][:, b : b + 1],
-                    scalar2=None, op0=ALU.mult,
-                )
+                live["rows", g, c] = rows_pool.tile([P, PACK, NODES], F32, name="rows_sb")
+            dst = live["rows", g, c][:, t, :]
+            src = live["adj", g][:, b, :]
+            r_j = live["r", g][:, b : b + 1]
+            if b == VECTOR_ROW_TILE or (g == 0 and 1 <= b <= 3):
+                nc.vector.tensor_scalar(out=dst, in0=src, scalar1=r_j, scalar2=None, op0=ALU.mult)
             else:
-                nc.scalar.activation(
-                    out=t1[:, t, :], in_=a_sb[g][:, b, :], func=ACT.Copy, scale=r_sb[g][:, b : b + 1]
-                )
+                nc.scalar.activation(out=dst, in_=src, func=ACT.Copy, scale=r_j)
 
-        def scale_cols(g, k):
+        def scale_columns(g, k):
             h = k // 2
             c = k % 2
-            ag = agpool.tile([P, HALF, 4], BF16, name="ag", align_bytes=64)
-            lo = HALF * h
+            unit = unit_pool.tile([P, HALF, PACK], BF16, name="unit_sb", align_bytes=64)
+            rows = live["rows", g, c][:, :, HALF * h : HALF * (h + 1)]
             nc.vector.tensor_tensor(
-                out=ag[:, 0:XV, :].rearrange("p (w i) t -> p w t i", i=4),
-                in0=t1_sb[(g, c)][:, :, lo : lo + XV].rearrange("p t (w i) -> p w t i", i=4),
-                in1=r_ps[(g, h)][:, 0:XV]
+                out=unit[:, 0:VECTOR_COLS, :].rearrange("p (w i) t -> p w t i", i=4),
+                in0=rows[:, :, 0:VECTOR_COLS].rearrange("p t (w i) -> p w t i", i=4),
+                in1=live["r_ps", g, h][:, 0:VECTOR_COLS]
                 .rearrange("p (w i) -> p w i", i=4)
                 .unsqueeze(2)
-                .to_broadcast([P, XV // 4, 4, 4]),
+                .to_broadcast([P, VECTOR_COLS // 4, PACK, 4]),
                 op=ALU.mult,
             )
             nc.gpsimd.tensor_tensor(
-                out=ag[:, XV:HALF, :],
-                in0=t1_sb[(g, c)][:, :, lo + XV : lo + HALF].rearrange("p t i -> p i t"),
-                in1=rg_sb[(g, h)][:].unsqueeze(2).to_broadcast([P, XG, 4]),
+                out=unit[:, VECTOR_COLS:HALF, :],
+                in0=rows[:, :, VECTOR_COLS:HALF].rearrange("p t i -> p i t"),
+                in1=live["r_sb", g, h][:].unsqueeze(2).to_broadcast([P, GPSIMD_COLS, PACK]),
                 op=ALU.mult,
             )
-            ag_sb[(g, k)] = ag
+            live["unit", g, k] = unit
 
-        def a_quant(g, k):
-            a_c = acpool.tile([P, HALF], U32, name="a_c", align_bytes=64)
-            a_s = acpool.tile([P, HALF], U8, name="a_s", align_bytes=64)
+        def quantise_a(g, k):
+            codes = aq_pool.tile([P, HALF], U32, name="a_codes", align_bytes=64)
+            scales = aq_pool.tile([P, HALF], U8, name="a_scales", align_bytes=64)
             nc.vector.quantize_mx(
-                out=a_c[:].bitcast(FP8X4), scales=a_s[:], in_=ag_sb[(g, k)][:].rearrange("p i t -> p (i t)")
+                out=codes[:].bitcast(FP8X4),
+                scales=scales[:],
+                in_=live["unit", g, k][:].rearrange("p i t -> p (i t)"),
             )
-            ac_sb[(g, k)] = (a_c, a_s)
+            live["aq", g, k] = (codes, scales)
 
-        def out_matmul(g, h):
-            hc, hs = hc_sb[g]
-            op = ps_ho.tile([P, 4, FH], F32, name="ho")
-            for k in range(4):
-                cols = slice(P * k, P * (k + 1))
+        def matmul_out(g, h):
+            h_codes, h_scales = live["hq", g]
+            bank = psum_mx.tile([P, PACK, F_HID], F32, name="mx_ps")
+            for tile_i in range(4):
+                nodes = slice(P * tile_i, P * (tile_i + 1))
                 for c in range(2):
-                    a_c, a_s = ac_sb[(g, 2 * h + c)]
+                    a_codes, a_scales = live["aq", g, 2 * h + c]
+                    feats = slice(F_HID * c, F_HID * (c + 1))
                     nc.tensor.matmul_mx(
-                        out=op[:, k, :],
-                        lhsT=a_c[:, cols].bitcast(FP8X4),
-                        lhsT_scale=a_s[:, cols],
-                        rhs=hc[:, FH * c : FH * (c + 1)].bitcast(FP8X4),
-                        rhs_scale=hs[:, FH * c : FH * (c + 1)],
+                        out=bank[:, tile_i, :],
+                        lhsT=a_codes[:, nodes].bitcast(FP8X4),
+                        lhsT_scale=a_scales[:, nodes],
+                        rhs=h_codes[:, feats].bitcast(FP8X4),
+                        rhs_scale=h_scales[:, feats],
                         start=(c == 0),
                         stop=(c == 1),
                     )
-            o_ps[(g, h)] = op
+            live["out_ps", g, h] = bank
 
-        def out_bias(g, h):
-            o_t = opool.tile([P, 4, FH], F32, name="o_sb")
+        def add_bias(g, h):
+            tile = out_pool.tile([P, 4, F_HID], F32, name="out_sb")
             nc.vector.tensor_tensor(
-                out=o_t[:], in0=o_ps[(g, h)][:], in1=b_f[:].unsqueeze(1).to_broadcast([P, 4, FH]), op=ALU.add
+                out=tile[:],
+                in0=live["out_ps", g, h][:],
+                in1=bias[:].unsqueeze(1).to_broadcast([P, 4, F_HID]),
+                op=ALU.add,
             )
-            o_sb[(g, h)] = o_t
+            live["out_sb", g, h] = tile
 
-        def out_relu_store(g, h):
-            o_t = o_sb[(g, h)]
-            nc.scalar.activation(out=o_t[:], in_=o_t[:], func=ACT.Relu)
+        def relu_store(g, h):
+            tile = live["out_sb", g, h]
+            nc.scalar.activation(out=tile[:], in_=tile[:], func=ACT.Relu)
             nc.sync.dma_start(
-                out=out[g, HALF * h : HALF * (h + 1), :].rearrange("(k p) f -> p k f", p=P), in_=o_t[:]
+                out=out[g, HALF * h : HALF * (h + 1), :].rearrange("(n p) f -> p n f", p=P), in_=tile[:]
             )
 
         load_x(0)
-        load_a(0)
-        load_a(1)
+        load_adj(0)
+        load_adj(1)
         load_x(1)
-        load_a(2)
-        w_raw = const.tile([P, 4, FH], BF16)
+        load_adj(2)
+        w_rows = const.tile([P, PACK, F_HID], BF16)
         nc.scalar.dma_start(
-            out=w_raw[:].rearrange("q (u e) f -> q u (e f)", u=2),
+            out=w_rows[:].rearrange("q (u e) f -> q u (e f)", u=2),
             in_=W1.rearrange("(u q e) f -> q u (e f)", u=2, e=2),
         )
-        b_bf = const.tile([P, FH], BF16)
-        nc.scalar.dma_start(out=b_bf[:], in_=b1.partition_broadcast(P))
+        bias_bf = const.tile([P, F_HID], BF16)
+        nc.scalar.dma_start(out=bias_bf[:], in_=b1.partition_broadcast(P))
         ident = const.tile([P, P], F32)
         make_identity(nc, ident[:])
-        ones = const.tile([P, 2], BF16)
+        ones = const.tile([P, 1], BF16)
         nc.vector.memset(ones[:], 1.0)
-        warm = const.tile([P, 1], F32)
-        nc.vector.memset(warm[:], 1.0)
-        nc.scalar.activation(out=warm[:], in_=warm[:], func=ACT.Sqrt)
-        w_grp = const.tile([P, FH, 4], BF16, align_bytes=64)
-        nc.vector.tensor_copy(out=w_grp[:], in_=w_raw[:].rearrange("q t f -> q f t"))
-        b_f = const.tile([P, FH], F32)
-        nc.vector.tensor_copy(out=b_f[:], in_=b_bf[:])
-        w_c = const.tile([P, FH], U32, align_bytes=64)
-        w_s = const.tile([P, FH], U8, align_bytes=64)
+        first_sqrt = const.tile([P, 1], F32)
+        nc.vector.memset(first_sqrt[:], 1.0)
+        nc.scalar.activation(out=first_sqrt[:], in_=first_sqrt[:], func=ACT.Sqrt)
+        w_grouped = const.tile([P, F_HID, PACK], BF16, align_bytes=64)
+        nc.vector.tensor_copy(out=w_grouped[:], in_=w_rows[:].rearrange("q t f -> q f t"))
+        bias = const.tile([P, F_HID], F32)
+        nc.vector.tensor_copy(out=bias[:], in_=bias_bf[:])
+        w_codes = const.tile([P, F_HID], U32, align_bytes=64)
+        w_scales = const.tile([P, F_HID], U8, align_bytes=64)
         nc.vector.quantize_mx(
-            out=w_c[:].bitcast(FP8X4), scales=w_s[:], in_=w_grp[:].rearrange("q f t -> q (f t)")
+            out=w_codes[:].bitcast(FP8X4), scales=w_scales[:], in_=w_grouped[:].rearrange("q f t -> q (f t)")
         )
 
         for s in range(4):
-            x_transpose(0, s)
-            x_copy(0, s)
-        x_quant(0)
-        colsum(0, 0, NB)
-        chain_a(0)
-        chain_s(0)
-        chain_b(0)
-        spread(0, 0)
-        spread(0, 1)
-        for b in range(NB):
+            transpose_x(0, s)
+            copy_x(0, s)
+        quantise_x(0)
+        column_sums(0, 0, ROW_TILES)
+        inv_sqrt_start(0)
+        inv_sqrt_root(0)
+        inv_sqrt_finish(0)
+        spread_r(0, 0)
+        spread_r(0, 1)
+        for b in range(0, 4):
             scale_rows(0, b)
-        spread_copy(0, 0)
-        spread_copy(0, 1)
+        copy_spread_r(0, 0)
+        copy_spread_r(0, 1)
+        for b in range(4, ROW_TILES):
+            scale_rows(0, b)
 
-        def later(g):
-            return 1 <= g < G
+        def is_graph(g):
+            return 0 <= g < GRAPHS
 
-        for g in range(-1, G + 1):
-            if ok(g):
-                h_matmul(g, 0)
-                h_matmul(g, 1)
-            if later(g):
-                spread(g, 1)
-            if later(g + 1):
-                x_transpose(g + 1, 0)
-                x_transpose(g + 1, 1)
-            if ok(g + 2):
-                colsum(g + 2, 0, 4)
-            if later(g):
+        def after_first(g):
+            return 1 <= g < GRAPHS
+
+        for g in range(-1, GRAPHS + 1):
+            if after_first(g):
+                spread_r(g, 1)
+            if after_first(g + 1):
+                transpose_x(g + 1, 0)
+                transpose_x(g + 1, 1)
+            if is_graph(g):
+                matmul_h(g, 0)
+                matmul_h(g, 1)
+            if is_graph(g + 2):
+                column_sums(g + 2, 0, 4)
+            if after_first(g):
                 scale_rows(g, 6)
-            if ok(g):
-                scale_cols(g, 0)
-            if later(g + 1):
-                chain_a(g + 1)
-                chain_s(g + 1)
-                x_copy(g + 1, 0)
-                x_copy(g + 1, 1)
-            if later(g):
-                spread_copy(g, 1)
-            if ok(g - 1):
-                out_bias(g - 1, 0)
-            if later(g):
+            if is_graph(g):
+                scale_columns(g, 0)
+            if after_first(g + 1):
+                inv_sqrt_start(g + 1)
+                inv_sqrt_root(g + 1)
+                copy_x(g + 1, 0)
+                copy_x(g + 1, 1)
+            if after_first(g):
+                copy_spread_r(g, 1)
                 scale_rows(g, 7)
-            if later(g + 1):
-                chain_b(g + 1)
-            if ok(g - 1):
-                a_quant(g - 1, 3)
-            if g >= 0 and ok(g + 2):
+            if after_first(g + 1):
+                inv_sqrt_finish(g + 1)
+            if is_graph(g - 1):
+                quantise_a(g - 1, 3)
+                add_bias(g - 1, 0)
+            if g >= 0 and is_graph(g + 2):
                 load_x(g + 2)
-            if g >= 0 and ok(g + 3):
-                load_a(g + 3)
-            if ok(g - 1):
-                out_matmul(g - 1, 1)
-            if ok(g + 2):
-                colsum(g + 2, 4, NB)
-            if later(g + 1):
+            if g >= 0 and is_graph(g + 3):
+                load_adj(g + 3)
+            if is_graph(g - 1):
+                matmul_out(g - 1, 1)
+            if is_graph(g + 2):
+                column_sums(g + 2, 4, ROW_TILES)
+            if after_first(g + 1):
                 scale_rows(g + 1, 0)
                 scale_rows(g + 1, 1)
-            if ok(g):
-                h_copy(g, 0)
-                h_copy(g, 1)
-                scale_cols(g, 1)
-            if later(g + 1):
-                scale_rows(g + 1, 3)
-            if ok(g):
-                a_quant(g, 0)
-            if later(g + 1):
-                spread(g + 1, 0)
-                x_transpose(g + 1, 2)
-                x_transpose(g + 1, 3)
+            if is_graph(g):
+                copy_h(g, 0)
+                copy_h(g, 1)
+                scale_columns(g, 1)
+                quantise_a(g, 0)
+            if after_first(g + 1):
+                spread_r(g + 1, 0)
+                transpose_x(g + 1, 2)
+                transpose_x(g + 1, 3)
                 scale_rows(g + 1, 2)
-                x_copy(g + 1, 2)
-                x_copy(g + 1, 3)
-            if ok(g - 1):
-                out_relu_store(g - 1, 0)
-            if ok(g):
-                scale_cols(g, 2)
-                h_quant(g)
-            if ok(g - 1):
-                out_bias(g - 1, 1)
-            if ok(g):
-                a_quant(g, 1)
-            if ok(g):
-                out_matmul(g, 0)
-            if later(g + 1):
+                scale_rows(g + 1, 3)
+                copy_x(g + 1, 2)
+                copy_x(g + 1, 3)
+            if is_graph(g - 1):
+                relu_store(g - 1, 0)
+            if is_graph(g):
+                scale_columns(g, 2)
+                quantise_h(g)
+                quantise_a(g, 1)
+            if is_graph(g - 1):
+                add_bias(g - 1, 1)
+            if is_graph(g):
+                matmul_out(g, 0)
+            if after_first(g + 1):
                 scale_rows(g + 1, 4)
                 scale_rows(g + 1, 5)
-                spread_copy(g + 1, 0)
-            if ok(g - 1):
-                out_relu_store(g - 1, 1)
-            if ok(g):
-                scale_cols(g, 3)
-            if later(g + 1):
-                x_quant(g + 1)
-            if ok(g):
-                a_quant(g, 2)
+                copy_spread_r(g + 1, 0)
+            if is_graph(g - 1):
+                relu_store(g - 1, 1)
+            if is_graph(g):
+                scale_columns(g, 3)
+            if after_first(g + 1):
+                quantise_x(g + 1)
+            if is_graph(g):
+                quantise_a(g, 2)

@@ -19,9 +19,9 @@ F_IN = 512
 F_HID = 128
 ROW_TILES = NODES // P
 HALF = 512
-GPSIMD_COLS = 128
-VECTOR_COLS = HALF - GPSIMD_COLS
-VECTOR_ROW_TILE = 7
+GPSIMD_COLS = 256
+VECTOR_COLS = NODES - GPSIMD_COLS
+TINY = 2.0**-100
 FLOPS = 2 * GRAPHS * NODES * F_IN * F_HID + 2 * GRAPHS * NODES * NODES * F_HID
 
 
@@ -33,8 +33,8 @@ def tile_gcn_pa_t_kernel(tc, batch_graph, adj, W1, b1, out):
         x_pool = ctx.enter_context(tc.tile_pool(name="x_pool", bufs=2))
         xq_pool = ctx.enter_context(tc.tile_pool(name="xq_pool", bufs=2))
         rows_pool = ctx.enter_context(tc.tile_pool(name="rows_pool", bufs=3))
-        unit_pool = ctx.enter_context(tc.tile_pool(name="unit_pool", bufs=2))
-        aq_pool = ctx.enter_context(tc.tile_pool(name="aq_pool", bufs=8))
+        pass_pool = ctx.enter_context(tc.tile_pool(name="pass_pool", bufs=2))
+        aq_pool = ctx.enter_context(tc.tile_pool(name="aq_pool", bufs=4))
         h_pool = ctx.enter_context(tc.tile_pool(name="h_pool", bufs=3))
         small = ctx.enter_context(tc.tile_pool(name="small", bufs=3))
         out_pool = ctx.enter_context(tc.tile_pool(name="out_pool", bufs=3))
@@ -46,11 +46,12 @@ def tile_gcn_pa_t_kernel(tc, batch_graph, adj, W1, b1, out):
 
         live = {}
 
-        def load_adj(g):
+        def load_adj(g, tiles_each):
             tile = adj_pool.tile([P, ROW_TILES, NODES], BF16, name="adj_sb")
             rows = adj[g].rearrange("(b p) i -> p b i", p=P)
-            for c in range(2):
-                nc.sync.dma_start(out=tile[:, 4 * c : 4 * c + 4, :], in_=rows[:, 4 * c : 4 * c + 4, :])
+            for first in range(0, ROW_TILES, tiles_each):
+                some = slice(first, first + tiles_each)
+                nc.sync.dma_start(out=tile[:, some, :], in_=rows[:, some, :])
             live["adj", g] = tile
 
         def load_x(g):
@@ -113,61 +114,72 @@ def tile_gcn_pa_t_kernel(tc, batch_graph, adj, W1, b1, out):
             )
             live["hq", g] = (codes, scales)
 
-        def column_sums(g, first, last):
-            if first == 0:
-                live["sum", g] = psum_sum.tile([P, ROW_TILES], F32, name="sum_ps")
-            for b in range(first, last):
-                for rows in range(ROW_TILES):
-                    nc.tensor.matmul(
-                        out=live["sum", g][:, b : b + 1],
-                        lhsT=live["adj", g][:, rows, P * b : P * (b + 1)],
-                        rhs=ones[:],
-                        start=(rows == 0),
-                        stop=(rows == ROW_TILES - 1),
-                    )
+        def sum_rows(out_column, g, b, first, last):
+            for rows in range(first, last):
+                nc.tensor.matmul(
+                    out=out_column,
+                    lhsT=live["adj", g][:, rows, P * b : P * (b + 1)],
+                    rhs=ones[:],
+                    start=(rows == first),
+                    stop=(rows == last - 1),
+                )
 
-        def inv_sqrt_start(g):
-            positive = small.tile([P, ROW_TILES], F32, name="positive")
-            nc.vector.tensor_single_scalar(out=positive[:], in_=live["sum", g][:], scalar=0.0, op=ALU.is_gt)
-            minus_safe = small.tile([P, ROW_TILES], F32, name="minus_safe")
-            nc.vector.scalar_tensor_tensor(
-                out=minus_safe[:],
-                in0=positive[:],
-                scalar=1.0,
-                in1=live["sum", g][:],
-                op0=ALU.subtract,
-                op1=ALU.subtract,
+        def column_sums(g):
+            sums = psum_sum.tile([P, 2 * ROW_TILES], F32, name="sum_ps")
+            for b in range(ROW_TILES):
+                sum_rows(sums[:, b : b + 1], g, b, 0, ROW_TILES)
+            live["sum", g] = sums[:, 0:ROW_TILES]
+
+        def column_sums_in_two_parts(g, split):
+            sums = psum_sum.tile([P, 2 * ROW_TILES], F32, name="sum_ps")
+            for b in range(ROW_TILES):
+                sum_rows(sums[:, b : b + 1], g, b, 0, split)
+            first_part = small.tile([P, ROW_TILES], F32, name="first_part")
+            nc.vector.tensor_copy(out=first_part[:], in_=sums[:, 0:ROW_TILES])
+            for b in range(ROW_TILES):
+                column = ROW_TILES + b
+                sum_rows(sums[:, column : column + 1], g, b, split, ROW_TILES)
+            total = small.tile([P, ROW_TILES], F32, name="total")
+            nc.vector.tensor_tensor(
+                out=total[:], in0=sums[:, ROW_TILES : 2 * ROW_TILES], in1=first_part[:], op=ALU.add
             )
-            live["positive", g] = positive
-            live["minus_safe", g] = minus_safe
+            live["sum", g] = total[:]
 
-        def inv_sqrt_root(g):
-            root = small.tile([P, ROW_TILES], F32, name="root")
-            nc.scalar.activation(out=root[:], in_=live["minus_safe", g][:], func=ACT.Sqrt, scale=-1.0)
-            live["root", g] = root
+        def root(g):
+            tile = small.tile([P, ROW_TILES], F32, name="root")
+            nc.scalar.activation(out=tile[:], in_=live["sum", g], func=ACT.Sqrt, bias=tiny[:])
+            live["root", g] = tile
 
-        def inv_sqrt_finish(g):
+        def invert_root(g):
             inverse = small.tile([P, ROW_TILES], F32, name="inverse")
             nc.vector.reciprocal(out=inverse[:], in_=live["root", g][:])
             r = small.tile([P, ROW_TILES], F32, name="r")
-            nc.vector.tensor_tensor(out=r[:], in0=inverse[:], in1=live["positive", g][:], op=ALU.mult)
+            nc.vector.scalar_tensor_tensor(
+                out=r[:],
+                in0=live["sum", g],
+                scalar=0.0,
+                in1=inverse[:],
+                op0=ALU.is_gt,
+                op1=ALU.mult,
+            )
             live["r", g] = r
 
-        def spread_r(g, h):
-            bank = psum_r.tile([P, HALF], F32, name="r_ps%d" % h)
-            for t in range(PACK):
-                b = PACK * h + t
-                nc.tensor.transpose(
-                    bank[:, P * t : P * (t + 1)], live["r", g][:, b : b + 1].to_broadcast([P, P]), ident[:]
-                )
-            live["r_ps", g, h] = bank
+        def spread_r(g):
+            for h in range(2):
+                bank = psum_r.tile([P, HALF], F32, name="r_ps%d" % h)
+                for t in range(PACK):
+                    b = PACK * h + t
+                    nc.tensor.transpose(
+                        bank[:, P * t : P * (t + 1)], live["r", g][:, b : b + 1].to_broadcast([P, P]), ident[:]
+                    )
+                live["r_ps", g, h] = bank
 
-        def copy_spread_r(g, h):
-            tile = small.tile([P, GPSIMD_COLS], F32, name="r_sb%d" % h)
-            nc.scalar.copy(out=tile[:], in_=live["r_ps", g, h][:, VECTOR_COLS:HALF])
-            live["r_sb", g, h] = tile
+        def copy_spread_r(g):
+            tile = small.tile([P, GPSIMD_COLS], F32, name="r_sb")
+            nc.scalar.copy(out=tile[:], in_=live["r_ps", g, 1][:, HALF - GPSIMD_COLS : HALF])
+            live["r_sb", g] = tile
 
-        def scale_rows(g, b):
+        def scale_rows(engine, g, b):
             c = b // PACK
             t = b % PACK
             if t == 0:
@@ -175,50 +187,57 @@ def tile_gcn_pa_t_kernel(tc, batch_graph, adj, W1, b1, out):
             dst = live["rows", g, c][:, t, :]
             src = live["adj", g][:, b, :]
             r_j = live["r", g][:, b : b + 1]
-            if b == VECTOR_ROW_TILE or (g == 0 and 1 <= b <= 3):
+            if engine == "scalar":
+                nc.scalar.activation(out=dst, in_=src, func=ACT.Copy, scale=r_j)
+            elif engine == "vector":
                 nc.vector.tensor_scalar(out=dst, in0=src, scalar1=r_j, scalar2=None, op0=ALU.mult)
             else:
-                nc.scalar.activation(out=dst, in_=src, func=ACT.Copy, scale=r_j)
+                nc.gpsimd.tensor_scalar(
+                    out=dst, in0=src, scalar1=r_j, scalar2=0.0, op0=ALU.mult, op1=ALU.add
+                )
 
-        def scale_columns(g, k):
-            h = k // 2
-            c = k % 2
-            unit = unit_pool.tile([P, HALF, PACK], BF16, name="unit_sb", align_bytes=64)
-            rows = live["rows", g, c][:, :, HALF * h : HALF * (h + 1)]
-            nc.vector.tensor_tensor(
-                out=unit[:, 0:VECTOR_COLS, :].rearrange("p (w i) t -> p w t i", i=4),
-                in0=rows[:, :, 0:VECTOR_COLS].rearrange("p t (w i) -> p w t i", i=4),
-                in1=live["r_ps", g, h][:, 0:VECTOR_COLS]
-                .rearrange("p (w i) -> p w i", i=4)
-                .unsqueeze(2)
-                .to_broadcast([P, VECTOR_COLS // 4, PACK, 4]),
-                op=ALU.mult,
-            )
+        def scale_columns(g, c):
+            tile = pass_pool.tile([P, NODES, PACK], BF16, name="pass_sb", align_bytes=64)
+            rows = live["rows", g, c]
             nc.gpsimd.tensor_tensor(
-                out=unit[:, VECTOR_COLS:HALF, :],
-                in0=rows[:, :, VECTOR_COLS:HALF].rearrange("p t i -> p i t"),
-                in1=live["r_sb", g, h][:].unsqueeze(2).to_broadcast([P, GPSIMD_COLS, PACK]),
+                out=tile[:, VECTOR_COLS:NODES, :],
+                in0=rows[:, :, VECTOR_COLS:NODES].rearrange("p t i -> p i t"),
+                in1=live["r_sb", g][:].unsqueeze(2).to_broadcast([P, GPSIMD_COLS, PACK]),
                 op=ALU.mult,
             )
-            live["unit", g, k] = unit
+            for h, first, last in ((0, 0, HALF), (1, HALF, VECTOR_COLS)):
+                width = last - first
+                nc.vector.tensor_tensor(
+                    out=tile[:, first:last, :].rearrange("p (w i) t -> p w t i", i=4),
+                    in0=rows[:, :, first:last].rearrange("p t (w i) -> p w t i", i=4),
+                    in1=live["r_ps", g, h][:, 0:width]
+                    .rearrange("p (w i) -> p w i", i=4)
+                    .unsqueeze(2)
+                    .to_broadcast([P, width // 4, PACK, 4]),
+                    op=ALU.mult,
+                )
+            live["pass", g, c] = tile
 
-        def quantise_a(g, k):
-            codes = aq_pool.tile([P, HALF], U32, name="a_codes", align_bytes=64)
-            scales = aq_pool.tile([P, HALF], U8, name="a_scales", align_bytes=64)
-            nc.vector.quantize_mx(
-                out=codes[:].bitcast(FP8X4),
-                scales=scales[:],
-                in_=live["unit", g, k][:].rearrange("p i t -> p (i t)"),
-            )
-            live["aq", g, k] = (codes, scales)
+        def quantise_a(g, c, pieces):
+            codes = aq_pool.tile([P, NODES], U32, name="a_codes", align_bytes=64)
+            scales = aq_pool.tile([P, NODES], U8, name="a_scales", align_bytes=64)
+            width = NODES // pieces
+            for first in range(0, NODES, width):
+                some = slice(first, first + width)
+                nc.vector.quantize_mx(
+                    out=codes[:, some].bitcast(FP8X4),
+                    scales=scales[:, some],
+                    in_=live["pass", g, c][:, some, :].rearrange("p i t -> p (i t)"),
+                )
+            live["aq", g, c] = (codes, scales)
 
         def matmul_out(g, h):
             h_codes, h_scales = live["hq", g]
             bank = psum_mx.tile([P, PACK, F_HID], F32, name="mx_ps")
             for tile_i in range(4):
-                nodes = slice(P * tile_i, P * (tile_i + 1))
+                nodes = slice(HALF * h + P * tile_i, HALF * h + P * (tile_i + 1))
                 for c in range(2):
-                    a_codes, a_scales = live["aq", g, 2 * h + c]
+                    a_codes, a_scales = live["aq", g, c]
                     feats = slice(F_HID * c, F_HID * (c + 1))
                     nc.tensor.matmul_mx(
                         out=bank[:, tile_i, :],
@@ -249,10 +268,10 @@ def tile_gcn_pa_t_kernel(tc, batch_graph, adj, W1, b1, out):
             )
 
         load_x(0)
-        load_adj(0)
-        load_adj(1)
+        load_adj(0, 2)
+        load_adj(1, 4)
         load_x(1)
-        load_adj(2)
+        load_adj(2, 4)
         w_rows = const.tile([P, PACK, F_HID], BF16)
         nc.scalar.dma_start(
             out=w_rows[:].rearrange("q (u e) f -> q u (e f)", u=2),
@@ -264,9 +283,10 @@ def tile_gcn_pa_t_kernel(tc, batch_graph, adj, W1, b1, out):
         make_identity(nc, ident[:])
         ones = const.tile([P, 1], BF16)
         nc.vector.memset(ones[:], 1.0)
-        first_sqrt = const.tile([P, 1], F32)
-        nc.vector.memset(first_sqrt[:], 1.0)
-        nc.scalar.activation(out=first_sqrt[:], in_=first_sqrt[:], func=ACT.Sqrt)
+        tiny = const.tile([P, 1], F32)
+        nc.vector.memset(tiny[:], TINY)
+        first_root = const.tile([P, 1], F32)
+        nc.scalar.activation(out=first_root[:], in_=tiny[:], func=ACT.Sqrt)
         w_grouped = const.tile([P, F_HID, PACK], BF16, align_bytes=64)
         nc.vector.tensor_copy(out=w_grouped[:], in_=w_rows[:].rearrange("q t f -> q f t"))
         bias = const.tile([P, F_HID], F32)
@@ -281,96 +301,80 @@ def tile_gcn_pa_t_kernel(tc, batch_graph, adj, W1, b1, out):
             transpose_x(0, s)
             copy_x(0, s)
         quantise_x(0)
-        column_sums(0, 0, ROW_TILES)
-        inv_sqrt_start(0)
-        inv_sqrt_root(0)
-        inv_sqrt_finish(0)
-        spread_r(0, 0)
-        spread_r(0, 1)
-        for b in range(0, 4):
-            scale_rows(0, b)
-        copy_spread_r(0, 0)
-        copy_spread_r(0, 1)
-        for b in range(4, ROW_TILES):
-            scale_rows(0, b)
+        column_sums_in_two_parts(0, 6)
+        root(0)
+        invert_root(0)
+        scale_rows("scalar", 0, 0)
+        scale_rows("vector", 0, 1)
+        scale_rows("vector", 0, 2)
+        scale_rows("vector", 0, 3)
+        spread_r(0)
+        copy_spread_r(0)
+        matmul_h(0, 0)
+        matmul_h(0, 1)
+        column_sums(1)
 
         def is_graph(g):
             return 0 <= g < GRAPHS
 
-        def after_first(g):
-            return 1 <= g < GRAPHS
-
-        for g in range(-1, GRAPHS + 1):
-            if after_first(g):
-                spread_r(g, 1)
-            if after_first(g + 1):
-                transpose_x(g + 1, 0)
-                transpose_x(g + 1, 1)
-            if is_graph(g):
-                matmul_h(g, 0)
-                matmul_h(g, 1)
-            if is_graph(g + 2):
-                column_sums(g + 2, 0, 4)
-            if after_first(g):
-                scale_rows(g, 6)
+        for g in range(GRAPHS + 2):
             if is_graph(g):
                 scale_columns(g, 0)
-            if after_first(g + 1):
-                inv_sqrt_start(g + 1)
-                inv_sqrt_root(g + 1)
-                copy_x(g + 1, 0)
-                copy_x(g + 1, 1)
-            if after_first(g):
-                copy_spread_r(g, 1)
-                scale_rows(g, 7)
-            if after_first(g + 1):
-                inv_sqrt_finish(g + 1)
-            if is_graph(g - 1):
-                quantise_a(g - 1, 3)
-                add_bias(g - 1, 0)
-            if g >= 0 and is_graph(g + 2):
-                load_x(g + 2)
-            if g >= 0 and is_graph(g + 3):
-                load_adj(g + 3)
-            if is_graph(g - 1):
-                matmul_out(g - 1, 1)
-            if is_graph(g + 2):
-                column_sums(g + 2, 4, ROW_TILES)
-            if after_first(g + 1):
-                scale_rows(g + 1, 0)
-                scale_rows(g + 1, 1)
+                scale_rows("scalar", g, 4)
+                scale_rows("scalar", g, 5)
+            if is_graph(g + 1):
+                root(g + 1)
             if is_graph(g):
                 copy_h(g, 0)
                 copy_h(g, 1)
+            if is_graph(g + 1):
+                transpose_x(g + 1, 0)
+                transpose_x(g + 1, 1)
+                copy_x(g + 1, 0)
+            if is_graph(g):
+                scale_rows("scalar", g, 6)
+                scale_rows("gpsimd", g, 7)
+            if is_graph(g + 1):
+                copy_x(g + 1, 1)
+            if g == GRAPHS:
+                quantise_a(g - 1, 1, 2)
+            if is_graph(g - 2):
+                add_bias(g - 2, 1)
+                relu_store(g - 2, 1)
+            if is_graph(g + 1):
+                invert_root(g + 1)
+            if is_graph(g):
+                quantise_h(g)
+            if is_graph(g - 1) and g < GRAPHS:
+                quantise_a(g - 1, 1, 1)
+            if is_graph(g + 2):
+                load_x(g + 2)
+            if is_graph(g + 3):
+                load_adj(g + 3, 4)
+            if is_graph(g - 1):
+                matmul_out(g - 1, 0)
+                matmul_out(g - 1, 1)
+            if is_graph(g):
                 scale_columns(g, 1)
-                quantise_a(g, 0)
-            if after_first(g + 1):
-                spread_r(g + 1, 0)
+            if is_graph(g + 1):
                 transpose_x(g + 1, 2)
                 transpose_x(g + 1, 3)
-                scale_rows(g + 1, 2)
-                scale_rows(g + 1, 3)
+                scale_rows("scalar", g + 1, 0)
                 copy_x(g + 1, 2)
                 copy_x(g + 1, 3)
+                scale_rows("scalar", g + 1, 1)
+                scale_rows("scalar", g + 1, 2)
+                scale_rows("gpsimd", g + 1, 3)
             if is_graph(g - 1):
+                add_bias(g - 1, 0)
                 relu_store(g - 1, 0)
-            if is_graph(g):
-                scale_columns(g, 2)
-                quantise_h(g)
-                quantise_a(g, 1)
-            if is_graph(g - 1):
-                add_bias(g - 1, 1)
-            if is_graph(g):
-                matmul_out(g, 0)
-            if after_first(g + 1):
-                scale_rows(g + 1, 4)
-                scale_rows(g + 1, 5)
-                copy_spread_r(g + 1, 0)
-            if is_graph(g - 1):
-                relu_store(g - 1, 1)
-            if is_graph(g):
-                scale_columns(g, 3)
-            if after_first(g + 1):
+            if is_graph(g + 1):
+                spread_r(g + 1)
+                copy_spread_r(g + 1)
                 quantise_x(g + 1)
+                matmul_h(g + 1, 0)
+                matmul_h(g + 1, 1)
+            if is_graph(g + 2):
+                column_sums(g + 2)
             if is_graph(g):
-                quantise_a(g, 2)
+                quantise_a(g, 0, 1)

@@ -21,6 +21,7 @@ ROW_TILES = NODES // P
 HALF = 512
 GPSIMD_COLS = 256
 VECTOR_COLS = NODES - GPSIMD_COLS
+GPSIMD_R = 2 * ROW_TILES
 TINY = 2.0**-100
 FLOPS = 2 * GRAPHS * NODES * F_IN * F_HID + 2 * GRAPHS * NODES * NODES * F_HID
 
@@ -125,13 +126,14 @@ def tile_gcn_pa_t_kernel(tc, batch_graph, adj, W1, b1, out):
                 )
 
         def column_sums(g):
-            sums = psum_sum.tile([P, 2 * ROW_TILES], F32, name="sum_ps")
+            sums = psum_sum.tile([P, HALF], F32, name="sum_ps")
             for b in range(ROW_TILES):
                 sum_rows(sums[:, b : b + 1], g, b, 0, ROW_TILES)
+            live["sum_bank", g] = sums
             live["sum", g] = sums[:, 0:ROW_TILES]
 
         def column_sums_in_two_parts(g, split):
-            sums = psum_sum.tile([P, 2 * ROW_TILES], F32, name="sum_ps")
+            sums = psum_sum.tile([P, HALF], F32, name="sum_ps")
             for b in range(ROW_TILES):
                 sum_rows(sums[:, b : b + 1], g, b, 0, split)
             first_part = small.tile([P, ROW_TILES], F32, name="first_part")
@@ -143,6 +145,7 @@ def tile_gcn_pa_t_kernel(tc, batch_graph, adj, W1, b1, out):
             nc.vector.tensor_tensor(
                 out=total[:], in0=sums[:, ROW_TILES : 2 * ROW_TILES], in1=first_part[:], op=ALU.add
             )
+            live["sum_bank", g] = sums
             live["sum", g] = total[:]
 
         def root(g):
@@ -153,30 +156,39 @@ def tile_gcn_pa_t_kernel(tc, batch_graph, adj, W1, b1, out):
         def invert_root(g):
             inverse = small.tile([P, ROW_TILES], F32, name="inverse")
             nc.vector.reciprocal(out=inverse[:], in_=live["root", g][:])
+            live["inverse", g] = inverse
+
+        def mask_r(g):
             r = small.tile([P, ROW_TILES], F32, name="r")
             nc.vector.scalar_tensor_tensor(
                 out=r[:],
                 in0=live["sum", g],
                 scalar=0.0,
-                in1=inverse[:],
+                in1=live["inverse", g][:],
                 op0=ALU.is_gt,
                 op1=ALU.mult,
             )
             live["r", g] = r
 
+        def spread_block(block, g, b):
+            nc.tensor.transpose(block, live["r", g][:, b : b + 1].to_broadcast([P, P]), ident[:])
+
         def spread_r(g):
             for h in range(2):
                 bank = psum_r.tile([P, HALF], F32, name="r_ps%d" % h)
-                for t in range(PACK):
-                    b = PACK * h + t
-                    nc.tensor.transpose(
-                        bank[:, P * t : P * (t + 1)], live["r", g][:, b : b + 1].to_broadcast([P, P]), ident[:]
-                    )
+                for b in range(PACK * h, min(PACK * (h + 1), VECTOR_COLS // P)):
+                    first = P * b - HALF * h
+                    spread_block(bank[:, first : first + P], g, b)
                 live["r_ps", g, h] = bank
 
-        def copy_spread_r(g):
+        def spread_gpsimd_r(g):
+            for b in range(VECTOR_COLS // P, ROW_TILES):
+                first = GPSIMD_R + P * b - VECTOR_COLS
+                spread_block(live["sum_bank", g][:, first : first + P], g, b)
+
+        def copy_gpsimd_r(g):
             tile = small.tile([P, GPSIMD_COLS], F32, name="r_sb")
-            nc.scalar.copy(out=tile[:], in_=live["r_ps", g, 1][:, HALF - GPSIMD_COLS : HALF])
+            nc.scalar.copy(out=tile[:], in_=live["sum_bank", g][:, GPSIMD_R : GPSIMD_R + GPSIMD_COLS])
             live["r_sb", g] = tile
 
         def scale_rows(engine, g, b):
@@ -304,12 +316,14 @@ def tile_gcn_pa_t_kernel(tc, batch_graph, adj, W1, b1, out):
         column_sums_in_two_parts(0, 6)
         root(0)
         invert_root(0)
+        mask_r(0)
         scale_rows("scalar", 0, 0)
         scale_rows("vector", 0, 1)
         scale_rows("vector", 0, 2)
         scale_rows("vector", 0, 3)
+        spread_gpsimd_r(0)
         spread_r(0)
-        copy_spread_r(0)
+        copy_gpsimd_r(0)
         matmul_h(0, 0)
         matmul_h(0, 1)
         column_sums(1)
@@ -338,11 +352,14 @@ def tile_gcn_pa_t_kernel(tc, batch_graph, adj, W1, b1, out):
                 copy_x(g + 1, 1)
             if g == GRAPHS:
                 quantise_a(g - 1, 1, 2)
+            if is_graph(g + 1):
+                invert_root(g + 1)
             if is_graph(g - 2):
                 add_bias(g - 2, 1)
                 relu_store(g - 2, 1)
             if is_graph(g + 1):
-                invert_root(g + 1)
+                mask_r(g + 1)
+                spread_gpsimd_r(g + 1)
             if is_graph(g):
                 quantise_h(g)
             if is_graph(g - 1) and g < GRAPHS:
@@ -360,6 +377,7 @@ def tile_gcn_pa_t_kernel(tc, batch_graph, adj, W1, b1, out):
                 transpose_x(g + 1, 2)
                 transpose_x(g + 1, 3)
                 scale_rows("scalar", g + 1, 0)
+                copy_gpsimd_r(g + 1)
                 copy_x(g + 1, 2)
                 copy_x(g + 1, 3)
                 scale_rows("scalar", g + 1, 1)
@@ -370,7 +388,6 @@ def tile_gcn_pa_t_kernel(tc, batch_graph, adj, W1, b1, out):
                 relu_store(g - 1, 0)
             if is_graph(g + 1):
                 spread_r(g + 1)
-                copy_spread_r(g + 1)
                 quantise_x(g + 1)
                 matmul_h(g + 1, 0)
                 matmul_h(g + 1, 1)

@@ -19,7 +19,7 @@ F_IN = 512
 F_HID = 128
 ROW_TILES = NODES // P
 HALF = 512
-GPSIMD_COLS = 256
+GPSIMD_COLS = 192
 VECTOR_COLS = NODES - GPSIMD_COLS
 GPSIMD_R = 2 * ROW_TILES
 TINY = 2.0**-100
@@ -176,19 +176,19 @@ def tile_gcn_pa_t_kernel(tc, batch_graph, adj, W1, b1, out):
         def spread_r(g):
             for h in range(2):
                 bank = psum_r.tile([P, HALF], F32, name="r_ps%d" % h)
-                for b in range(PACK * h, min(PACK * (h + 1), VECTOR_COLS // P)):
+                for b in range(PACK * h, min(PACK * (h + 1), (VECTOR_COLS + P - 1) // P)):
                     first = P * b - HALF * h
                     spread_block(bank[:, first : first + P], g, b)
                 live["r_ps", g, h] = bank
 
         def spread_gpsimd_r(g):
             for b in range(VECTOR_COLS // P, ROW_TILES):
-                first = GPSIMD_R + P * b - VECTOR_COLS
+                first = GPSIMD_R + P * b - P * (VECTOR_COLS // P)
                 spread_block(live["sum_bank", g][:, first : first + P], g, b)
 
         def copy_gpsimd_r(g):
             tile = small.tile([P, GPSIMD_COLS], F32, name="r_sb")
-            nc.scalar.copy(out=tile[:], in_=live["sum_bank", g][:, GPSIMD_R : GPSIMD_R + GPSIMD_COLS])
+            nc.scalar.copy(out=tile[:], in_=live["sum_bank", g][:, GPSIMD_R + VECTOR_COLS % P : GPSIMD_R + VECTOR_COLS % P + GPSIMD_COLS])
             live["r_sb", g] = tile
 
         def scale_rows(engine, g, b):

@@ -19,7 +19,7 @@ F_IN = 512
 F_HID = 128
 ROW_TILES = NODES // P
 HALF = 512
-GPSIMD_COLS = 192
+GPSIMD_COLS = 320
 VECTOR_COLS = NODES - GPSIMD_COLS
 GPSIMD_R = 2 * ROW_TILES
 TINY = 2.0**-100
@@ -125,12 +125,12 @@ def tile_gcn_pa_t_kernel(tc, batch_graph, adj, W1, b1, out):
                     stop=(rows == last - 1),
                 )
 
-        def column_sums(g):
-            sums = psum_sum.tile([P, HALF], F32, name="sum_ps")
-            for b in range(ROW_TILES):
-                sum_rows(sums[:, b : b + 1], g, b, 0, ROW_TILES)
-            live["sum_bank", g] = sums
-            live["sum", g] = sums[:, 0:ROW_TILES]
+        def column_sums(g, first, last):
+            if first == 0:
+                live["sum_bank", g] = psum_sum.tile([P, HALF], F32, name="sum_ps")
+                live["sum", g] = live["sum_bank", g][:, 0:ROW_TILES]
+            for b in range(first, last):
+                sum_rows(live["sum_bank", g][:, b : b + 1], g, b, 0, ROW_TILES)
 
         def column_sums_in_two_parts(g, split):
             sums = psum_sum.tile([P, HALF], F32, name="sum_ps")
@@ -217,31 +217,35 @@ def tile_gcn_pa_t_kernel(tc, batch_graph, adj, W1, b1, out):
                 in1=live["r_sb", g][:].unsqueeze(2).to_broadcast([P, GPSIMD_COLS, PACK]),
                 op=ALU.mult,
             )
-            for h, first, last in ((0, 0, HALF), (1, HALF, VECTOR_COLS)):
-                width = last - first
-                nc.vector.tensor_tensor(
-                    out=tile[:, first:last, :].rearrange("p (w i) t -> p w t i", i=4),
-                    in0=rows[:, :, first:last].rearrange("p t (w i) -> p w t i", i=4),
-                    in1=live["r_ps", g, h][:, 0:width]
-                    .rearrange("p (w i) -> p w i", i=4)
-                    .unsqueeze(2)
-                    .to_broadcast([P, width // 4, PACK, 4]),
-                    op=ALU.mult,
-                )
             live["pass", g, c] = tile
+            vector_columns(g, c, 0)
 
-        def quantise_a(g, c, pieces):
-            codes = aq_pool.tile([P, NODES], U32, name="a_codes", align_bytes=64)
-            scales = aq_pool.tile([P, NODES], U8, name="a_scales", align_bytes=64)
-            width = NODES // pieces
-            for first in range(0, NODES, width):
-                some = slice(first, first + width)
-                nc.vector.quantize_mx(
-                    out=codes[:, some].bitcast(FP8X4),
-                    scales=scales[:, some],
-                    in_=live["pass", g, c][:, some, :].rearrange("p i t -> p (i t)"),
-                )
-            live["aq", g, c] = (codes, scales)
+        def vector_columns(g, c, h):
+            first = HALF * h
+            last = min(first + HALF, VECTOR_COLS)
+            width = last - first
+            nc.vector.tensor_tensor(
+                out=live["pass", g, c][:, first:last, :].rearrange("p (w i) t -> p w t i", i=4),
+                in0=live["rows", g, c][:, :, first:last].rearrange("p t (w i) -> p w t i", i=4),
+                in1=live["r_ps", g, h][:, 0:width]
+                .rearrange("p (w i) -> p w i", i=4)
+                .unsqueeze(2)
+                .to_broadcast([P, width // 4, PACK, 4]),
+                op=ALU.mult,
+            )
+
+        def quantise_a(g, c, first=0, last=NODES):
+            if first == 0:
+                codes = aq_pool.tile([P, NODES], U32, name="a_codes", align_bytes=64)
+                scales = aq_pool.tile([P, NODES], U8, name="a_scales", align_bytes=64)
+                live["aq", g, c] = (codes, scales)
+            codes, scales = live["aq", g, c]
+            some = slice(first, last)
+            nc.vector.quantize_mx(
+                out=codes[:, some].bitcast(FP8X4),
+                scales=scales[:, some],
+                in_=live["pass", g, c][:, some, :].rearrange("p i t -> p (i t)"),
+            )
 
         def matmul_out(g, h):
             h_codes, h_scales = live["hq", g]
@@ -326,7 +330,7 @@ def tile_gcn_pa_t_kernel(tc, batch_graph, adj, W1, b1, out):
         copy_gpsimd_r(0)
         matmul_h(0, 0)
         matmul_h(0, 1)
-        column_sums(1)
+        column_sums(1, 0, ROW_TILES)
 
         def is_graph(g):
             return 0 <= g < GRAPHS
@@ -334,6 +338,7 @@ def tile_gcn_pa_t_kernel(tc, batch_graph, adj, W1, b1, out):
         for g in range(GRAPHS + 2):
             if is_graph(g):
                 scale_columns(g, 0)
+                vector_columns(g, 0, 1)
                 scale_rows("scalar", g, 4)
                 scale_rows("scalar", g, 5)
             if is_graph(g + 1):
@@ -345,13 +350,13 @@ def tile_gcn_pa_t_kernel(tc, batch_graph, adj, W1, b1, out):
                 transpose_x(g + 1, 0)
                 transpose_x(g + 1, 1)
                 copy_x(g + 1, 0)
+                copy_x(g + 1, 1)
             if is_graph(g):
                 scale_rows("scalar", g, 6)
                 scale_rows("gpsimd", g, 7)
-            if is_graph(g + 1):
-                copy_x(g + 1, 1)
             if g == GRAPHS:
-                quantise_a(g - 1, 1, 2)
+                quantise_a(g - 1, 1, 0, HALF)
+                vector_columns(g - 1, 1, 1)
             if is_graph(g + 1):
                 invert_root(g + 1)
             if is_graph(g - 2):
@@ -362,8 +367,13 @@ def tile_gcn_pa_t_kernel(tc, batch_graph, adj, W1, b1, out):
                 spread_gpsimd_r(g + 1)
             if is_graph(g):
                 quantise_h(g)
-            if is_graph(g - 1) and g < GRAPHS:
-                quantise_a(g - 1, 1, 1)
+            if g == GRAPHS:
+                quantise_a(g - 1, 1, HALF, NODES)
+            elif is_graph(g - 1):
+                quantise_a(g - 1, 1)
+            if is_graph(g + 1):
+                transpose_x(g + 1, 2)
+                transpose_x(g + 1, 3)
             if is_graph(g + 2):
                 load_x(g + 2)
             if is_graph(g + 3):
@@ -373,11 +383,14 @@ def tile_gcn_pa_t_kernel(tc, batch_graph, adj, W1, b1, out):
                 matmul_out(g - 1, 1)
             if is_graph(g):
                 scale_columns(g, 1)
+            if g + 1 < GRAPHS:
+                vector_columns(g, 1, 1)
             if is_graph(g + 1):
-                transpose_x(g + 1, 2)
-                transpose_x(g + 1, 3)
                 scale_rows("scalar", g + 1, 0)
                 copy_gpsimd_r(g + 1)
+            if is_graph(g + 2):
+                column_sums(g + 2, 0, 4)
+            if is_graph(g + 1):
                 copy_x(g + 1, 2)
                 copy_x(g + 1, 3)
                 scale_rows("scalar", g + 1, 1)
@@ -392,6 +405,6 @@ def tile_gcn_pa_t_kernel(tc, batch_graph, adj, W1, b1, out):
                 matmul_h(g + 1, 0)
                 matmul_h(g + 1, 1)
             if is_graph(g + 2):
-                column_sums(g + 2)
+                column_sums(g + 2, 4, ROW_TILES)
             if is_graph(g):
-                quantise_a(g, 0, 1)
+                quantise_a(g, 0)

@@ -19,9 +19,9 @@ F_IN = 512
 F_HID = 128
 ROW_TILES = NODES // P
 HALF = 512
-GPSIMD_COLS = 320
+GPSIMD_COLS = 256
 VECTOR_COLS = NODES - GPSIMD_COLS
-GPSIMD_R = 2 * ROW_TILES
+GPSIMD_R = ROW_TILES
 TINY = 2.0**-100
 FLOPS = 2 * GRAPHS * NODES * F_IN * F_HID + 2 * GRAPHS * NODES * NODES * F_HID
 
@@ -38,7 +38,7 @@ def tile_gcn_pa_t_kernel(tc, batch_graph, adj, W1, b1, out):
         aq_pool = ctx.enter_context(tc.tile_pool(name="aq_pool", bufs=4))
         h_pool = ctx.enter_context(tc.tile_pool(name="h_pool", bufs=3))
         small = ctx.enter_context(tc.tile_pool(name="small", bufs=3))
-        out_pool = ctx.enter_context(tc.tile_pool(name="out_pool", bufs=3))
+        out_pool = ctx.enter_context(tc.tile_pool(name="out_pool", bufs=5))
         psum_x = ctx.enter_context(tc.psum_pool(name="psum_x", bufs=2))
         psum_mx = ctx.enter_context(tc.psum_pool(name="psum_mx", bufs=3))
         psum_sum = ctx.enter_context(tc.psum_pool(name="psum_sum", bufs=1))
@@ -133,18 +133,16 @@ def tile_gcn_pa_t_kernel(tc, batch_graph, adj, W1, b1, out):
                 sum_rows(live["sum_bank", g][:, b : b + 1], g, b, 0, ROW_TILES)
 
         def column_sums_in_two_parts(g, split):
+            first_sums = psum_mx.tile([P, ROW_TILES], F32, name="mx_ps")
             sums = psum_sum.tile([P, HALF], F32, name="sum_ps")
             for b in range(ROW_TILES):
-                sum_rows(sums[:, b : b + 1], g, b, 0, split)
-            first_part = small.tile([P, ROW_TILES], F32, name="first_part")
-            nc.vector.tensor_copy(out=first_part[:], in_=sums[:, 0:ROW_TILES])
+                sum_rows(first_sums[:, b : b + 1], g, b, 0, split)
             for b in range(ROW_TILES):
-                column = ROW_TILES + b
-                sum_rows(sums[:, column : column + 1], g, b, split, ROW_TILES)
+                sum_rows(sums[:, b : b + 1], g, b, split, ROW_TILES)
+            first_part = small.tile([P, ROW_TILES], F32, name="first_part")
+            nc.vector.tensor_copy(out=first_part[:], in_=first_sums[:])
             total = small.tile([P, ROW_TILES], F32, name="total")
-            nc.vector.tensor_tensor(
-                out=total[:], in0=sums[:, ROW_TILES : 2 * ROW_TILES], in1=first_part[:], op=ALU.add
-            )
+            nc.vector.tensor_tensor(out=total[:], in0=sums[:, 0:ROW_TILES], in1=first_part[:], op=ALU.add)
             live["sum_bank", g] = sums
             live["sum", g] = total[:]
 
@@ -234,7 +232,7 @@ def tile_gcn_pa_t_kernel(tc, batch_graph, adj, W1, b1, out):
                 op=ALU.mult,
             )
 
-        def quantise_a(g, c, first=0, last=NODES):
+        def quantise_a(g, c, first, last):
             if first == 0:
                 codes = aq_pool.tile([P, NODES], U32, name="a_codes", align_bytes=64)
                 scales = aq_pool.tile([P, NODES], U8, name="a_scales", align_bytes=64)
@@ -247,11 +245,11 @@ def tile_gcn_pa_t_kernel(tc, batch_graph, adj, W1, b1, out):
                 in_=live["pass", g, c][:, some, :].rearrange("p i t -> p (i t)"),
             )
 
-        def matmul_out(g, h):
+        def matmul_out(g, first, tiles):
             h_codes, h_scales = live["hq", g]
             bank = psum_mx.tile([P, PACK, F_HID], F32, name="mx_ps")
-            for tile_i in range(4):
-                nodes = slice(HALF * h + P * tile_i, HALF * h + P * (tile_i + 1))
+            for tile_i in range(tiles):
+                nodes = slice(P * (first + tile_i), P * (first + tile_i + 1))
                 for c in range(2):
                     a_codes, a_scales = live["aq", g, c]
                     feats = slice(F_HID * c, F_HID * (c + 1))
@@ -264,23 +262,23 @@ def tile_gcn_pa_t_kernel(tc, batch_graph, adj, W1, b1, out):
                         start=(c == 0),
                         stop=(c == 1),
                     )
-            live["out_ps", g, h] = bank
+            live["out_ps", g, first] = bank
 
-        def add_bias(g, h):
-            tile = out_pool.tile([P, 4, F_HID], F32, name="out_sb")
+        def add_bias(g, first, tiles):
+            tile = out_pool.tile([P, tiles, F_HID], F32, name="out_sb")
             nc.vector.tensor_tensor(
                 out=tile[:],
-                in0=live["out_ps", g, h][:],
-                in1=bias[:].unsqueeze(1).to_broadcast([P, 4, F_HID]),
+                in0=live["out_ps", g, first][:, 0:tiles, :],
+                in1=bias[:].unsqueeze(1).to_broadcast([P, tiles, F_HID]),
                 op=ALU.add,
             )
-            live["out_sb", g, h] = tile
+            live["out_sb", g, first] = tile
 
-        def relu_store(g, h):
-            tile = live["out_sb", g, h]
+        def relu_store(g, first, tiles):
+            tile = live["out_sb", g, first]
             nc.scalar.activation(out=tile[:], in_=tile[:], func=ACT.Relu)
             nc.sync.dma_start(
-                out=out[g, HALF * h : HALF * (h + 1), :].rearrange("(n p) f -> p n f", p=P), in_=tile[:]
+                out=out[g, P * first : P * (first + tiles), :].rearrange("(n p) f -> p n f", p=P), in_=tile[:]
             )
 
         load_x(0)
@@ -317,7 +315,9 @@ def tile_gcn_pa_t_kernel(tc, batch_graph, adj, W1, b1, out):
             transpose_x(0, s)
             copy_x(0, s)
         quantise_x(0)
-        column_sums_in_two_parts(0, 6)
+        column_sums_in_two_parts(0, 4)
+        matmul_h(0, 0)
+        matmul_h(0, 1)
         root(0)
         invert_root(0)
         mask_r(0)
@@ -328,83 +328,96 @@ def tile_gcn_pa_t_kernel(tc, batch_graph, adj, W1, b1, out):
         spread_gpsimd_r(0)
         spread_r(0)
         copy_gpsimd_r(0)
-        matmul_h(0, 0)
-        matmul_h(0, 1)
         column_sums(1, 0, ROW_TILES)
 
-        def is_graph(g):
-            return 0 <= g < GRAPHS
-
-        for g in range(GRAPHS + 2):
-            if is_graph(g):
-                scale_columns(g, 0)
-                vector_columns(g, 0, 1)
-                scale_rows("scalar", g, 4)
-                scale_rows("scalar", g, 5)
-            if is_graph(g + 1):
+        for g in range(GRAPHS):
+            first = g == 0
+            scale_columns(g, 0)
+            vector_columns(g, 0, 1)
+            scale_rows("scalar", g, 4)
+            scale_rows("scalar", g, 5)
+            if first:
+                scale_rows("scalar", g, 6)
+                scale_rows("vector", g, 7)
+            if g + 1 < GRAPHS:
                 root(g + 1)
-            if is_graph(g):
+            if not first:
                 copy_h(g, 0)
                 copy_h(g, 1)
-            if is_graph(g + 1):
+            if g + 1 < GRAPHS:
                 transpose_x(g + 1, 0)
                 transpose_x(g + 1, 1)
                 copy_x(g + 1, 0)
                 copy_x(g + 1, 1)
-            if is_graph(g):
+            if not first:
                 scale_rows("scalar", g, 6)
                 scale_rows("gpsimd", g, 7)
-            if g == GRAPHS:
-                quantise_a(g - 1, 1, 0, HALF)
-                vector_columns(g - 1, 1, 1)
-            if is_graph(g + 1):
+            if g + 1 < GRAPHS:
                 invert_root(g + 1)
-            if is_graph(g - 2):
-                add_bias(g - 2, 1)
-                relu_store(g - 2, 1)
-            if is_graph(g + 1):
+            if g >= 2:
+                add_bias(g - 2, 4, 4)
+                relu_store(g - 2, 4, 4)
+            if g + 1 < GRAPHS:
                 mask_r(g + 1)
                 spread_gpsimd_r(g + 1)
-            if is_graph(g):
+            if not first:
+                quantise_a(g - 1, 1, 0, NODES)
                 quantise_h(g)
-            if g == GRAPHS:
-                quantise_a(g - 1, 1, HALF, NODES)
-            elif is_graph(g - 1):
-                quantise_a(g - 1, 1)
-            if is_graph(g + 1):
+            if g + 1 < GRAPHS:
                 transpose_x(g + 1, 2)
                 transpose_x(g + 1, 3)
-            if is_graph(g + 2):
+            if g + 2 < GRAPHS:
                 load_x(g + 2)
-            if is_graph(g + 3):
+            if g + 3 < GRAPHS:
                 load_adj(g + 3, 4)
-            if is_graph(g - 1):
-                matmul_out(g - 1, 0)
-                matmul_out(g - 1, 1)
-            if is_graph(g):
-                scale_columns(g, 1)
+            if not first:
+                matmul_out(g - 1, 0, 4)
+                matmul_out(g - 1, 4, 4)
+            scale_columns(g, 1)
             if g + 1 < GRAPHS:
                 vector_columns(g, 1, 1)
-            if is_graph(g + 1):
+            if first:
+                copy_h(g, 0)
+                copy_h(g, 1)
+            if g + 1 < GRAPHS:
                 scale_rows("scalar", g + 1, 0)
                 copy_gpsimd_r(g + 1)
-            if is_graph(g + 2):
+            if g + 2 < GRAPHS:
                 column_sums(g + 2, 0, 4)
-            if is_graph(g + 1):
+            if g + 1 < GRAPHS:
                 copy_x(g + 1, 2)
                 copy_x(g + 1, 3)
                 scale_rows("scalar", g + 1, 1)
                 scale_rows("scalar", g + 1, 2)
                 scale_rows("gpsimd", g + 1, 3)
-            if is_graph(g - 1):
-                add_bias(g - 1, 0)
-                relu_store(g - 1, 0)
-            if is_graph(g + 1):
+            if not first:
+                add_bias(g - 1, 0, 4)
+                relu_store(g - 1, 0, 4)
+            if g + 1 < GRAPHS:
                 spread_r(g + 1)
+            if g + 2 < GRAPHS:
+                column_sums(g + 2, 4, ROW_TILES)
+            if first:
+                quantise_h(g)
+            quantise_a(g, 0, 0, NODES)
+            if g + 1 < GRAPHS:
                 quantise_x(g + 1)
                 matmul_h(g + 1, 0)
                 matmul_h(g + 1, 1)
-            if is_graph(g + 2):
-                column_sums(g + 2, 4, ROW_TILES)
-            if is_graph(g):
-                quantise_a(g, 0)
+
+        g = GRAPHS - 1
+        quantise_a(g, 1, 0, HALF)
+        vector_columns(g, 1, 1)
+        matmul_out(g, 0, 4)
+        add_bias(g - 1, 4, 4)
+        relu_store(g - 1, 4, 4)
+        quantise_a(g, 1, HALF, HALF + 2 * P)
+        quantise_a(g, 1, HALF + 2 * P, NODES)
+        matmul_out(g, 4, 2)
+        add_bias(g, 0, 4)
+        relu_store(g, 0, 4)
+        matmul_out(g, 6, 2)
+        add_bias(g, 4, 2)
+        relu_store(g, 4, 2)
+        add_bias(g, 6, 2)
+        relu_store(g, 6, 2)

@@ -132,18 +132,24 @@ def tile_gcn_pa_t_kernel(tc, batch_graph, adj, W1, b1, out):
             for b in range(first, last):
                 sum_rows(live["sum_bank", g][:, b : b + 1], g, b, 0, ROW_TILES)
 
-        def column_sums_in_two_parts(g, split):
-            first_sums = psum_mx.tile([P, ROW_TILES], F32, name="mx_ps")
-            sums = psum_sum.tile([P, HALF], F32, name="sum_ps")
-            for b in range(ROW_TILES):
-                sum_rows(first_sums[:, b : b + 1], g, b, 0, split)
-            for b in range(ROW_TILES):
-                sum_rows(sums[:, b : b + 1], g, b, split, ROW_TILES)
-            first_part = small.tile([P, ROW_TILES], F32, name="first_part")
-            nc.vector.tensor_copy(out=first_part[:], in_=first_sums[:])
-            total = small.tile([P, ROW_TILES], F32, name="total")
-            nc.vector.tensor_tensor(out=total[:], in0=sums[:, 0:ROW_TILES], in1=first_part[:], op=ALU.add)
-            live["sum_bank", g] = sums
+        def column_sums_in_parts(g, ends):
+            live["sum_bank", g] = psum_sum.tile([P, HALF], F32, name="sum_ps")
+            begin = 0
+            total = None
+            for end in ends:
+                if end == ROW_TILES:
+                    sums = live["sum_bank", g]
+                else:
+                    sums = psum_mx.tile([P, ROW_TILES], F32, name="mx_ps")
+                for b in range(ROW_TILES):
+                    sum_rows(sums[:, b : b + 1], g, b, begin, end)
+                so_far = small.tile([P, ROW_TILES], F32, name="so_far")
+                if begin == 0:
+                    nc.vector.tensor_copy(out=so_far[:], in_=sums[:, 0:ROW_TILES])
+                else:
+                    nc.vector.tensor_tensor(out=so_far[:], in0=sums[:, 0:ROW_TILES], in1=total[:], op=ALU.add)
+                total = so_far
+                begin = end
             live["sum", g] = total[:]
 
         def root(g):
@@ -281,18 +287,18 @@ def tile_gcn_pa_t_kernel(tc, batch_graph, adj, W1, b1, out):
                 out=out[g, P * first : P * (first + tiles), :].rearrange("(n p) f -> p n f", p=P), in_=tile[:]
             )
 
-        load_x(0)
         load_adj(0, 2)
         load_adj(1, 4)
-        load_x(1)
+        load_x(0)
         load_adj(2, 4)
+        load_x(1)
+        bias = const.tile([P, F_HID], BF16)
+        nc.sync.dma_start(out=bias[:], in_=b1.partition_broadcast(P))
         w_rows = const.tile([P, PACK, F_HID], BF16)
         nc.scalar.dma_start(
             out=w_rows[:].rearrange("q (u e) f -> q u (e f)", u=2),
             in_=W1.rearrange("(u q e) f -> q u (e f)", u=2, e=2),
         )
-        bias_bf = const.tile([P, F_HID], BF16)
-        nc.scalar.dma_start(out=bias_bf[:], in_=b1.partition_broadcast(P))
         ident = const.tile([P, P], F32)
         make_identity(nc, ident[:])
         ones = const.tile([P, 1], BF16)
@@ -303,21 +309,13 @@ def tile_gcn_pa_t_kernel(tc, batch_graph, adj, W1, b1, out):
         nc.scalar.activation(out=first_root[:], in_=tiny[:], func=ACT.Sqrt)
         w_grouped = const.tile([P, F_HID, PACK], BF16, align_bytes=64)
         nc.vector.tensor_copy(out=w_grouped[:], in_=w_rows[:].rearrange("q t f -> q f t"))
-        bias = const.tile([P, F_HID], F32)
-        nc.vector.tensor_copy(out=bias[:], in_=bias_bf[:])
         w_codes = const.tile([P, F_HID], U32, align_bytes=64)
         w_scales = const.tile([P, F_HID], U8, align_bytes=64)
         nc.vector.quantize_mx(
             out=w_codes[:].bitcast(FP8X4), scales=w_scales[:], in_=w_grouped[:].rearrange("q f t -> q (f t)")
         )
 
-        for s in range(4):
-            transpose_x(0, s)
-            copy_x(0, s)
-        quantise_x(0)
-        column_sums_in_two_parts(0, 4)
-        matmul_h(0, 0)
-        matmul_h(0, 1)
+        column_sums_in_parts(0, (4, 6, 8))
         root(0)
         invert_root(0)
         mask_r(0)
@@ -332,6 +330,7 @@ def tile_gcn_pa_t_kernel(tc, batch_graph, adj, W1, b1, out):
 
         for g in range(GRAPHS):
             first = g == 0
+            last = g == GRAPHS - 1
             scale_columns(g, 0)
             vector_columns(g, 0, 1)
             scale_rows("scalar", g, 4)
@@ -342,13 +341,17 @@ def tile_gcn_pa_t_kernel(tc, batch_graph, adj, W1, b1, out):
             if g + 1 < GRAPHS:
                 root(g + 1)
             if not first:
-                copy_h(g, 0)
-                copy_h(g, 1)
-            if g + 1 < GRAPHS:
-                transpose_x(g + 1, 0)
-                transpose_x(g + 1, 1)
-                copy_x(g + 1, 0)
-                copy_x(g + 1, 1)
+                copy_h(g - 1, 0)
+                copy_h(g - 1, 1)
+            transpose_x(g, 0)
+            transpose_x(g, 1)
+            copy_x(g, 0)
+            copy_x(g, 1)
+            if last:
+                transpose_x(g, 2)
+                transpose_x(g, 3)
+                copy_x(g, 2)
+                copy_x(g, 3)
             if not first:
                 scale_rows("scalar", g, 6)
                 scale_rows("gpsimd", g, 7)
@@ -360,12 +363,19 @@ def tile_gcn_pa_t_kernel(tc, batch_graph, adj, W1, b1, out):
             if g + 1 < GRAPHS:
                 mask_r(g + 1)
                 spread_gpsimd_r(g + 1)
-            if not first:
+            if last:
+                quantise_h(g - 1)
+                quantise_x(g)
                 quantise_a(g - 1, 1, 0, NODES)
-                quantise_h(g)
-            if g + 1 < GRAPHS:
-                transpose_x(g + 1, 2)
-                transpose_x(g + 1, 3)
+            elif not first:
+                quantise_a(g - 1, 1, 0, NODES)
+                quantise_h(g - 1)
+            if last:
+                matmul_h(g, 0)
+                matmul_h(g, 1)
+            else:
+                transpose_x(g, 2)
+                transpose_x(g, 3)
             if g + 2 < GRAPHS:
                 load_x(g + 2)
             if g + 3 < GRAPHS:
@@ -376,17 +386,16 @@ def tile_gcn_pa_t_kernel(tc, batch_graph, adj, W1, b1, out):
             scale_columns(g, 1)
             if g + 1 < GRAPHS:
                 vector_columns(g, 1, 1)
-            if first:
-                copy_h(g, 0)
-                copy_h(g, 1)
-            if g + 1 < GRAPHS:
                 scale_rows("scalar", g + 1, 0)
                 copy_gpsimd_r(g + 1)
             if g + 2 < GRAPHS:
                 column_sums(g + 2, 0, 4)
-            if g + 1 < GRAPHS:
-                copy_x(g + 1, 2)
-                copy_x(g + 1, 3)
+            if last:
+                copy_h(g, 0)
+                copy_h(g, 1)
+            else:
+                copy_x(g, 2)
+                copy_x(g, 3)
                 scale_rows("scalar", g + 1, 1)
                 scale_rows("scalar", g + 1, 2)
                 scale_rows("gpsimd", g + 1, 3)
@@ -397,20 +406,20 @@ def tile_gcn_pa_t_kernel(tc, batch_graph, adj, W1, b1, out):
                 spread_r(g + 1)
             if g + 2 < GRAPHS:
                 column_sums(g + 2, 4, ROW_TILES)
-            if first:
-                quantise_h(g)
             quantise_a(g, 0, 0, NODES)
-            if g + 1 < GRAPHS:
-                quantise_x(g + 1)
-                matmul_h(g + 1, 0)
-                matmul_h(g + 1, 1)
+            if last:
+                quantise_h(g)
+            else:
+                quantise_x(g)
+                matmul_h(g, 0)
+                matmul_h(g, 1)
 
         g = GRAPHS - 1
         quantise_a(g, 1, 0, HALF)
         vector_columns(g, 1, 1)
-        matmul_out(g, 0, 4)
         add_bias(g - 1, 4, 4)
         relu_store(g - 1, 4, 4)
+        matmul_out(g, 0, 4)
         quantise_a(g, 1, HALF, HALF + 2 * P)
         quantise_a(g, 1, HALF + 2 * P, NODES)
         matmul_out(g, 4, 2)

@@ -288,17 +288,17 @@ def tile_gcn_pa_t_kernel(tc, batch_graph, adj, W1, b1, out):
             )
 
         load_adj(0, 2)
+        w_rows = const.tile([P, PACK, F_HID], BF16)
+        nc.sync.dma_start(
+            out=w_rows[:].rearrange("q (u e) f -> q u (e f)", u=2),
+            in_=W1.rearrange("(u q e) f -> q u (e f)", u=2, e=2),
+        )
         load_adj(1, 4)
         load_x(0)
         load_adj(2, 4)
         load_x(1)
         bias = const.tile([P, F_HID], BF16)
         nc.sync.dma_start(out=bias[:], in_=b1.partition_broadcast(P))
-        w_rows = const.tile([P, PACK, F_HID], BF16)
-        nc.scalar.dma_start(
-            out=w_rows[:].rearrange("q (u e) f -> q u (e f)", u=2),
-            in_=W1.rearrange("(u q e) f -> q u (e f)", u=2, e=2),
-        )
         ident = const.tile([P, P], F32)
         make_identity(nc, ident[:])
         ones = const.tile([P, 1], BF16)
@@ -307,6 +307,8 @@ def tile_gcn_pa_t_kernel(tc, batch_graph, adj, W1, b1, out):
         nc.vector.memset(tiny[:], TINY)
         first_root = const.tile([P, 1], F32)
         nc.scalar.activation(out=first_root[:], in_=tiny[:], func=ACT.Sqrt)
+        column_sums_in_parts(0, (4, 6, 8))
+        root(0)
         w_grouped = const.tile([P, F_HID, PACK], BF16, align_bytes=64)
         nc.vector.tensor_copy(out=w_grouped[:], in_=w_rows[:].rearrange("q t f -> q f t"))
         w_codes = const.tile([P, F_HID], U32, align_bytes=64)
@@ -314,9 +316,6 @@ def tile_gcn_pa_t_kernel(tc, batch_graph, adj, W1, b1, out):
         nc.vector.quantize_mx(
             out=w_codes[:].bitcast(FP8X4), scales=w_scales[:], in_=w_grouped[:].rearrange("q f t -> q (f t)")
         )
-
-        column_sums_in_parts(0, (4, 6, 8))
-        root(0)
         invert_root(0)
         mask_r(0)
         scale_rows("scalar", 0, 0)
@@ -333,28 +332,37 @@ def tile_gcn_pa_t_kernel(tc, batch_graph, adj, W1, b1, out):
             last = g == GRAPHS - 1
             scale_columns(g, 0)
             vector_columns(g, 0, 1)
-            scale_rows("scalar", g, 4)
-            scale_rows("scalar", g, 5)
-            if first:
-                scale_rows("scalar", g, 6)
-                scale_rows("vector", g, 7)
-            if g + 1 < GRAPHS:
-                root(g + 1)
-            if not first:
-                copy_h(g - 1, 0)
-                copy_h(g - 1, 1)
-            transpose_x(g, 0)
-            transpose_x(g, 1)
-            copy_x(g, 0)
-            copy_x(g, 1)
             if last:
+                copy_x(g, 0)
+                copy_x(g, 1)
+                scale_rows("scalar", g, 4)
                 transpose_x(g, 2)
                 transpose_x(g, 3)
                 copy_x(g, 2)
                 copy_x(g, 3)
-            if not first:
+                copy_h(g - 1, 0)
+                copy_h(g - 1, 1)
+                scale_rows("scalar", g, 5)
                 scale_rows("scalar", g, 6)
                 scale_rows("gpsimd", g, 7)
+            else:
+                scale_rows("scalar", g, 4)
+                scale_rows("scalar", g, 5)
+                if first:
+                    scale_rows("scalar", g, 6)
+                    scale_rows("vector", g, 7)
+                root(g + 1)
+                if first:
+                    transpose_x(g, 0)
+                    transpose_x(g, 1)
+                else:
+                    copy_h(g - 1, 0)
+                    copy_h(g - 1, 1)
+                copy_x(g, 0)
+                copy_x(g, 1)
+                if not first:
+                    scale_rows("scalar", g, 6)
+                    scale_rows("gpsimd", g, 7)
             if g + 1 < GRAPHS:
                 invert_root(g + 1)
             if g >= 2:
@@ -364,9 +372,9 @@ def tile_gcn_pa_t_kernel(tc, batch_graph, adj, W1, b1, out):
                 mask_r(g + 1)
                 spread_gpsimd_r(g + 1)
             if last:
-                quantise_h(g - 1)
                 quantise_x(g)
                 quantise_a(g - 1, 1, 0, NODES)
+                quantise_h(g - 1)
             elif not first:
                 quantise_a(g - 1, 1, 0, NODES)
                 quantise_h(g - 1)
@@ -411,6 +419,8 @@ def tile_gcn_pa_t_kernel(tc, batch_graph, adj, W1, b1, out):
                 quantise_h(g)
             else:
                 quantise_x(g)
+                transpose_x(g + 1, 0)
+                transpose_x(g + 1, 1)
                 matmul_h(g, 0)
                 matmul_h(g, 1)
 

@@ -38,6 +38,7 @@ def tile_gcn_pa_t_kernel(tc, batch_graph, adj, W1, b1, out):
         aq_pool = ctx.enter_context(tc.tile_pool(name="aq_pool", bufs=4))
         h_pool = ctx.enter_context(tc.tile_pool(name="h_pool", bufs=3))
         small = ctx.enter_context(tc.tile_pool(name="small", bufs=3))
+        turn_pool = ctx.enter_context(tc.tile_pool(name="turn_pool", bufs=2))
         out_pool = ctx.enter_context(tc.tile_pool(name="out_pool", bufs=5))
         psum_x = ctx.enter_context(tc.psum_pool(name="psum_x", bufs=2))
         psum_mx = ctx.enter_context(tc.psum_pool(name="psum_mx", bufs=3))
@@ -212,17 +213,14 @@ def tile_gcn_pa_t_kernel(tc, batch_graph, adj, W1, b1, out):
                     out=dst, in0=src, scalar1=r_j, scalar2=0.0, op0=ALU.mult, op1=ALU.add
                 )
 
-        def scale_columns(g, c):
-            tile = pass_pool.tile([P, NODES, PACK], BF16, name="pass_sb", align_bytes=64)
-            rows = live["rows", g, c]
+        def gpsimd_columns(g, c):
+            live["pass", g, c] = pass_pool.tile([P, NODES, PACK], BF16, name="pass_sb", align_bytes=64)
             nc.gpsimd.tensor_tensor(
-                out=tile[:, VECTOR_COLS:NODES, :],
-                in0=rows[:, :, VECTOR_COLS:NODES].rearrange("p t i -> p i t"),
+                out=live["pass", g, c][:, VECTOR_COLS:NODES, :],
+                in0=live["rows", g, c][:, :, VECTOR_COLS:NODES].rearrange("p t i -> p i t"),
                 in1=live["r_sb", g][:].unsqueeze(2).to_broadcast([P, GPSIMD_COLS, PACK]),
                 op=ALU.mult,
             )
-            live["pass", g, c] = tile
-            vector_columns(g, c, 0)
 
         def vector_columns(g, c, h):
             first = HALF * h
@@ -236,6 +234,36 @@ def tile_gcn_pa_t_kernel(tc, batch_graph, adj, W1, b1, out):
                 .unsqueeze(2)
                 .to_broadcast([P, width // 4, PACK, 4]),
                 op=ALU.mult,
+            )
+
+        def turn_rows(g, c, b):
+            bank = psum_x.tile([P, PACK, P], F32, name="xT_ps")
+            for t in range(PACK):
+                nc.tensor.transpose(bank[:, t, :], live["rows", g, c][:, t, P * b : P * (b + 1)], ident[:])
+            live["turned_ps", g, b] = bank
+
+        def scale_turned(g, b):
+            tile = turn_pool.tile([P, PACK * P], BF16, name="turned")
+            nc.scalar.activation(
+                out=tile[:].rearrange("p (u q e) -> p u q e", u=2, e=2),
+                in_=live["turned_ps", g, b][:].rearrange("p (u e) q -> p u q e", e=2),
+                func=ACT.Copy,
+                scale=live["r", g][:, b : b + 1],
+            )
+            live["turned", g, b] = tile
+
+        def turn_back(g, b):
+            words = live["turned", g, b][:].bitcast(F32)
+            bank = psum_x.tile([P, 2, P], F32, name="xT_ps")
+            for u in range(2):
+                nc.tensor.transpose(bank[:, u, :], words[:, P * u : P * (u + 1)], ident[:])
+            live["back_ps", g, b] = bank
+
+        def copy_turned(g, c, b):
+            block = live["pass", g, c][:, P * b : P * (b + 1), :].rearrange("p i t -> p (i t)")
+            nc.scalar.copy(
+                out=block.bitcast(F32).rearrange("p (i u) -> p i u", u=2),
+                in_=live["back_ps", g, b][:].rearrange("p u i -> p i u"),
             )
 
         def quantise_a(g, c, first, last):
@@ -288,17 +316,17 @@ def tile_gcn_pa_t_kernel(tc, batch_graph, adj, W1, b1, out):
             )
 
         load_adj(0, 2)
-        w_rows = const.tile([P, PACK, F_HID], BF16)
-        nc.sync.dma_start(
-            out=w_rows[:].rearrange("q (u e) f -> q u (e f)", u=2),
-            in_=W1.rearrange("(u q e) f -> q u (e f)", u=2, e=2),
-        )
         load_adj(1, 4)
         load_x(0)
         load_adj(2, 4)
         load_x(1)
         bias = const.tile([P, F_HID], BF16)
         nc.sync.dma_start(out=bias[:], in_=b1.partition_broadcast(P))
+        w_rows = const.tile([P, PACK, F_HID], BF16)
+        nc.scalar.dma_start(
+            out=w_rows[:].rearrange("q (u e) f -> q u (e f)", u=2),
+            in_=W1.rearrange("(u q e) f -> q u (e f)", u=2, e=2),
+        )
         ident = const.tile([P, P], F32)
         make_identity(nc, ident[:])
         ones = const.tile([P, 1], BF16)
@@ -307,8 +335,6 @@ def tile_gcn_pa_t_kernel(tc, batch_graph, adj, W1, b1, out):
         nc.vector.memset(tiny[:], TINY)
         first_root = const.tile([P, 1], F32)
         nc.scalar.activation(out=first_root[:], in_=tiny[:], func=ACT.Sqrt)
-        column_sums_in_parts(0, (4, 6, 8))
-        root(0)
         w_grouped = const.tile([P, F_HID, PACK], BF16, align_bytes=64)
         nc.vector.tensor_copy(out=w_grouped[:], in_=w_rows[:].rearrange("q t f -> q f t"))
         w_codes = const.tile([P, F_HID], U32, align_bytes=64)
@@ -316,6 +342,9 @@ def tile_gcn_pa_t_kernel(tc, batch_graph, adj, W1, b1, out):
         nc.vector.quantize_mx(
             out=w_codes[:].bitcast(FP8X4), scales=w_scales[:], in_=w_grouped[:].rearrange("q f t -> q (f t)")
         )
+
+        column_sums_in_parts(0, (4, 6, 8))
+        root(0)
         invert_root(0)
         mask_r(0)
         scale_rows("scalar", 0, 0)
@@ -330,7 +359,8 @@ def tile_gcn_pa_t_kernel(tc, batch_graph, adj, W1, b1, out):
         for g in range(GRAPHS):
             first = g == 0
             last = g == GRAPHS - 1
-            scale_columns(g, 0)
+            gpsimd_columns(g, 0)
+            vector_columns(g, 0, 0)
             vector_columns(g, 0, 1)
             if last:
                 copy_x(g, 0)
@@ -388,48 +418,59 @@ def tile_gcn_pa_t_kernel(tc, batch_graph, adj, W1, b1, out):
                 load_x(g + 2)
             if g + 3 < GRAPHS:
                 load_adj(g + 3, 4)
+            if last:
+                break
             if not first:
                 matmul_out(g - 1, 0, 4)
                 matmul_out(g - 1, 4, 4)
-            scale_columns(g, 1)
-            if g + 1 < GRAPHS:
-                vector_columns(g, 1, 1)
-                scale_rows("scalar", g + 1, 0)
-                copy_gpsimd_r(g + 1)
+            gpsimd_columns(g, 1)
+            vector_columns(g, 1, 0)
+            vector_columns(g, 1, 1)
+            scale_rows("scalar", g + 1, 0)
+            copy_gpsimd_r(g + 1)
             if g + 2 < GRAPHS:
                 column_sums(g + 2, 0, 4)
-            if last:
-                copy_h(g, 0)
-                copy_h(g, 1)
-            else:
-                copy_x(g, 2)
-                copy_x(g, 3)
-                scale_rows("scalar", g + 1, 1)
-                scale_rows("scalar", g + 1, 2)
-                scale_rows("gpsimd", g + 1, 3)
+            copy_x(g, 2)
+            copy_x(g, 3)
+            scale_rows("scalar", g + 1, 1)
+            scale_rows("scalar", g + 1, 2)
+            scale_rows("gpsimd", g + 1, 3)
             if not first:
                 add_bias(g - 1, 0, 4)
                 relu_store(g - 1, 0, 4)
-            if g + 1 < GRAPHS:
-                spread_r(g + 1)
+            spread_r(g + 1)
             if g + 2 < GRAPHS:
                 column_sums(g + 2, 4, ROW_TILES)
             quantise_a(g, 0, 0, NODES)
-            if last:
-                quantise_h(g)
-            else:
-                quantise_x(g)
-                transpose_x(g + 1, 0)
-                transpose_x(g + 1, 1)
-                matmul_h(g, 0)
-                matmul_h(g, 1)
+            quantise_x(g)
+            transpose_x(g + 1, 0)
+            transpose_x(g + 1, 1)
+            matmul_h(g, 0)
+            matmul_h(g, 1)
 
         g = GRAPHS - 1
+        matmul_out(g - 1, 0, 4)
+        gpsimd_columns(g, 1)
+        vector_columns(g, 1, 0)
+        copy_h(g, 0)
+        copy_h(g, 1)
+        turn_rows(g, 1, 4)
+        scale_turned(g, 4)
+        turn_rows(g, 1, 5)
+        scale_turned(g, 5)
+        turn_back(g, 4)
+        copy_turned(g, 1, 4)
+        turn_back(g, 5)
+        copy_turned(g, 1, 5)
+        matmul_out(g - 1, 4, 4)
+        add_bias(g - 1, 0, 4)
+        relu_store(g - 1, 0, 4)
+        quantise_a(g, 0, 0, NODES)
+        quantise_h(g)
         quantise_a(g, 1, 0, HALF)
-        vector_columns(g, 1, 1)
+        matmul_out(g, 0, 4)
         add_bias(g - 1, 4, 4)
         relu_store(g - 1, 4, 4)
-        matmul_out(g, 0, 4)
         quantise_a(g, 1, HALF, HALF + 2 * P)
         quantise_a(g, 1, HALF + 2 * P, NODES)
         matmul_out(g, 4, 2)

from contextlib import ExitStack

import concourse.mybir as mybir
from concourse.masks import make_identity

F32 = mybir.dt.float32
BF16 = mybir.dt.bfloat16
U32 = mybir.dt.uint32
U8 = mybir.dt.uint8
FP8X4 = mybir.dt.float8_e4m3fn_x4
ALU = mybir.AluOpType
ACT = mybir.ActivationFunctionType

P = 128
PACK = 4
GRAPHS = 8
NODES = 1024
F_IN = 512
F_HID = 128
ROW_TILES = NODES // P
HALF = 512
GPSIMD_COLS = 256
VECTOR_COLS = NODES - GPSIMD_COLS
GPSIMD_R = ROW_TILES
TINY = 2.0**-100
FLOPS = 2 * GRAPHS * NODES * F_IN * F_HID + 2 * GRAPHS * NODES * NODES * F_HID


def tile_gcn_pa_t_kernel(tc, batch_graph, adj, W1, b1, out):
    nc = tc.nc
    with ExitStack() as ctx:
        const = ctx.enter_context(tc.tile_pool(name="const", bufs=1))
        adj_pool = ctx.enter_context(tc.tile_pool(name="adj_pool", bufs=3))
        x_pool = ctx.enter_context(tc.tile_pool(name="x_pool", bufs=2))
        xq_pool = ctx.enter_context(tc.tile_pool(name="xq_pool", bufs=2))
        rows_pool = ctx.enter_context(tc.tile_pool(name="rows_pool", bufs=3))
        pass_pool = ctx.enter_context(tc.tile_pool(name="pass_pool", bufs=2))
        aq_pool = ctx.enter_context(tc.tile_pool(name="aq_pool", bufs=4))
        h_pool = ctx.enter_context(tc.tile_pool(name="h_pool", bufs=3))
        small = ctx.enter_context(tc.tile_pool(name="small", bufs=3))
        turn_pool = ctx.enter_context(tc.tile_pool(name="turn_pool", bufs=2))
        out_pool = ctx.enter_context(tc.tile_pool(name="out_pool", bufs=5))
        psum_x = ctx.enter_context(tc.psum_pool(name="psum_x", bufs=2))
        psum_mx = ctx.enter_context(tc.psum_pool(name="psum_mx", bufs=3))
        psum_sum = ctx.enter_context(tc.psum_pool(name="psum_sum", bufs=1))
        psum_r = ctx.enter_context(tc.psum_pool(name="psum_r", bufs=1))
        ctx.enter_context(tc.manual_schedule())

        live = {}

        def load_adj(g, tiles_each):
            tile = adj_pool.tile([P, ROW_TILES, NODES], BF16, name="adj_sb")
            rows = adj[g].rearrange("(b p) i -> p b i", p=P)
            for first in range(0, ROW_TILES, tiles_each):
                some = slice(first, first + tiles_each)
                nc.sync.dma_start(out=tile[:, some, :], in_=rows[:, some, :])
            live["adj", g] = tile

        def load_x(g):
            tile = x_pool.tile([P, ROW_TILES * F_IN], BF16, name="x_sb")
            nc.sync.dma_start(
                out=tile[:].rearrange("p (b k) -> p b k", b=ROW_TILES),
                in_=batch_graph[g].rearrange("(b p) k -> p b k", p=P),
            )
            live["x", g] = tile

        def transpose_x(g, s):
            words = live["x", g][:].bitcast(F32)
            bank = psum_x.tile([P, 2, 2, P], F32, name="xT_ps")
            for b2 in range(2):
                for u in range(2):
                    first = (F_IN // 2) * (2 * s + b2) + P * u
                    nc.tensor.transpose(bank[:, b2, u, :], words[:, first : first + P], ident[:])
            live["xT", g, s] = bank

        def copy_x(g, s):
            if s == 0:
                live["xg", g] = xq_pool.tile([P, PACK * NODES], BF16, name="x_grouped", align_bytes=64)
            grouped = live["xg", g][:].bitcast(F32).rearrange("q (s b n u) -> q s b n u", s=4, b=2, u=2)
            nc.scalar.copy(out=grouped[:, s], in_=live["xT", g, s][:].rearrange("q b u n -> q b n u"))

        def quantise_x(g):
            codes = xq_pool.tile([P, NODES], U32, name="x_codes", align_bytes=64)
            scales = xq_pool.tile([P, NODES], U8, name="x_scales", align_bytes=64)
            nc.vector.quantize_mx(out=codes[:].bitcast(FP8X4), scales=scales[:], in_=live["xg", g][:])
            live["xq", g] = (codes, scales)

        def matmul_h(g, c):
            codes, scales = live["xq", g]
            bank = psum_mx.tile([P, PACK, F_HID], F32, name="mx_ps")
            for t in range(PACK):
                nodes = slice(P * (PACK * c + t), P * (PACK * c + t + 1))
                nc.tensor.matmul_mx(
                    out=bank[:, t, :],
                    lhsT=codes[:, nodes].bitcast(FP8X4),
                    lhsT_scale=scales[:, nodes],
                    rhs=w_codes[:].bitcast(FP8X4),
                    rhs_scale=w_scales[:],
                    start=True,
                    stop=True,
                )
            live["h_ps", g, c] = bank

        def copy_h(g, c):
            if c == 0:
                live["hg", g] = h_pool.tile([P, 2, F_HID, PACK], BF16, name="h_grouped", align_bytes=64)
            nc.scalar.copy(out=live["hg", g][:, c], in_=live["h_ps", g, c][:].rearrange("p t f -> p f t"))

        def quantise_h(g):
            codes = h_pool.tile([P, 2 * F_HID], U32, name="h_codes", align_bytes=64)
            scales = h_pool.tile([P, 2 * F_HID], U8, name="h_scales", align_bytes=64)
            nc.vector.quantize_mx(
                out=codes[:].bitcast(FP8X4),
                scales=scales[:],
                in_=live["hg", g][:].rearrange("p c f t -> p (c f t)"),
            )
            live["hq", g] = (codes, scales)

        def sum_rows(out_column, g, b, first, last):
            for rows in range(first, last):
                nc.tensor.matmul(
                    out=out_column,
                    lhsT=live["adj", g][:, rows, P * b : P * (b + 1)],
                    rhs=ones[:],
                    start=(rows == first),
                    stop=(rows == last - 1),
                )

        def column_sums(g, first, last):
            if first == 0:
                live["sum_bank", g] = psum_sum.tile([P, HALF], F32, name="sum_ps")
                live["sum", g] = live["sum_bank", g][:, 0:ROW_TILES]
            for b in range(first, last):
                sum_rows(live["sum_bank", g][:, b : b + 1], g, b, 0, ROW_TILES)

        def column_sums_in_parts(g, ends):
            live["sum_bank", g] = psum_sum.tile([P, HALF], F32, name="sum_ps")
            begin = 0
            total = None
            for end in ends:
                if end == ROW_TILES:
                    sums = live["sum_bank", g]
                else:
                    sums = psum_mx.tile([P, ROW_TILES], F32, name="mx_ps")
                for b in range(ROW_TILES):
                    sum_rows(sums[:, b : b + 1], g, b, begin, end)
                so_far = small.tile([P, ROW_TILES], F32, name="so_far")
                if begin == 0:
                    nc.vector.tensor_copy(out=so_far[:], in_=sums[:, 0:ROW_TILES])
                else:
                    nc.vector.tensor_tensor(out=so_far[:], in0=sums[:, 0:ROW_TILES], in1=total[:], op=ALU.add)
                total = so_far
                begin = end
            live["sum", g] = total[:]

        def root(g):
            tile = small.tile([P, ROW_TILES], F32, name="root")
            nc.scalar.activation(out=tile[:], in_=live["sum", g], func=ACT.Sqrt, bias=tiny[:])
            live["root", g] = tile

        def invert_root(g):
            inverse = small.tile([P, ROW_TILES], F32, name="inverse")
            nc.vector.reciprocal(out=inverse[:], in_=live["root", g][:])
            live["inverse", g] = inverse

        def mask_r(g):
            r = small.tile([P, ROW_TILES], F32, name="r")
            nc.vector.scalar_tensor_tensor(
                out=r[:],
                in0=live["sum", g],
                scalar=0.0,
                in1=live["inverse", g][:],
                op0=ALU.is_gt,
                op1=ALU.mult,
            )
            live["r", g] = r

        def spread_block(block, g, b):
            nc.tensor.transpose(block, live["r", g][:, b : b + 1].to_broadcast([P, P]), ident[:])

        def spread_r(g):
            for h in range(2):
                bank = psum_r.tile([P, HALF], F32, name="r_ps%d" % h)
                for b in range(PACK * h, min(PACK * (h + 1), (VECTOR_COLS + P - 1) // P)):
                    first = P * b - HALF * h
                    spread_block(bank[:, first : first + P], g, b)
                live["r_ps", g, h] = bank

        def spread_gpsimd_r(g):
            for b in range(VECTOR_COLS // P, ROW_TILES):
                first = GPSIMD_R + P * b - P * (VECTOR_COLS // P)
                spread_block(live["sum_bank", g][:, first : first + P], g, b)

        def copy_gpsimd_r(g):
            tile = small.tile([P, GPSIMD_COLS], F32, name="r_sb")
            nc.scalar.copy(out=tile[:], in_=live["sum_bank", g][:, GPSIMD_R + VECTOR_COLS % P : GPSIMD_R + VECTOR_COLS % P + GPSIMD_COLS])
            live["r_sb", g] = tile

        def scale_rows(engine, g, b):
            c = b // PACK
            t = b % PACK
            if t == 0:
                live["rows", g, c] = rows_pool.tile([P, PACK, NODES], F32, name="rows_sb")
            dst = live["rows", g, c][:, t, :]
            src = live["adj", g][:, b, :]
            r_j = live["r", g][:, b : b + 1]
            if engine == "scalar":
                nc.scalar.activation(out=dst, in_=src, func=ACT.Copy, scale=r_j)
            elif engine == "vector":
                nc.vector.tensor_scalar(out=dst, in0=src, scalar1=r_j, scalar2=None, op0=ALU.mult)
            else:
                nc.gpsimd.tensor_scalar(
                    out=dst, in0=src, scalar1=r_j, scalar2=0.0, op0=ALU.mult, op1=ALU.add
                )

        def gpsimd_columns(g, c):
            live["pass", g, c] = pass_pool.tile([P, NODES, PACK], BF16, name="pass_sb", align_bytes=64)
            nc.gpsimd.tensor_tensor(
                out=live["pass", g, c][:, VECTOR_COLS:NODES, :],
                in0=live["rows", g, c][:, :, VECTOR_COLS:NODES].rearrange("p t i -> p i t"),
                in1=live["r_sb", g][:].unsqueeze(2).to_broadcast([P, GPSIMD_COLS, PACK]),
                op=ALU.mult,
            )

        def vector_columns(g, c, h):
            first = HALF * h
            last = min(first + HALF, VECTOR_COLS)
            width = last - first
            nc.vector.tensor_tensor(
                out=live["pass", g, c][:, first:last, :].rearrange("p (w i) t -> p w t i", i=4),
                in0=live["rows", g, c][:, :, first:last].rearrange("p t (w i) -> p w t i", i=4),
                in1=live["r_ps", g, h][:, 0:width]
                .rearrange("p (w i) -> p w i", i=4)
                .unsqueeze(2)
                .to_broadcast([P, width // 4, PACK, 4]),
                op=ALU.mult,
            )

        def turn_rows(g, c, b):
            bank = psum_x.tile([P, PACK, P], F32, name="xT_ps")
            for t in range(PACK):
                nc.tensor.transpose(bank[:, t, :], live["rows", g, c][:, t, P * b : P * (b + 1)], ident[:])
            live["turned_ps", g, b] = bank

        def scale_turned(g, b):
            tile = turn_pool.tile([P, PACK * P], BF16, name="turned")
            nc.scalar.activation(
                out=tile[:].rearrange("p (u q e) -> p u q e", u=2, e=2),
                in_=live["turned_ps", g, b][:].rearrange("p (u e) q -> p u q e", e=2),
                func=ACT.Copy,
                scale=live["r", g][:, b : b + 1],
            )
            live["turned", g, b] = tile

        def turn_back(g, b):
            words = live["turned", g, b][:].bitcast(F32)
            bank = psum_x.tile([P, 2, P], F32, name="xT_ps")
            for u in range(2):
                nc.tensor.transpose(bank[:, u, :], words[:, P * u : P * (u + 1)], ident[:])
            live["back_ps", g, b] = bank

        def copy_turned(g, c, b):
            block = live["pass", g, c][:, P * b : P * (b + 1), :].rearrange("p i t -> p (i t)")
            nc.scalar.copy(
                out=block.bitcast(F32).rearrange("p (i u) -> p i u", u=2),
                in_=live["back_ps", g, b][:].rearrange("p u i -> p i u"),
            )

        def quantise_a(g, c, first, last):
            if first == 0:
                codes = aq_pool.tile([P, NODES], U32, name="a_codes", align_bytes=64)
                scales = aq_pool.tile([P, NODES], U8, name="a_scales", align_bytes=64)
                live["aq", g, c] = (codes, scales)
            codes, scales = live["aq", g, c]
            some = slice(first, last)
            nc.vector.quantize_mx(
                out=codes[:, some].bitcast(FP8X4),
                scales=scales[:, some],
                in_=live["pass", g, c][:, some, :].rearrange("p i t -> p (i t)"),
            )

        def matmul_out(g, first, tiles):
            h_codes, h_scales = live["hq", g]
            bank = psum_mx.tile([P, PACK, F_HID], F32, name="mx_ps")
            for tile_i in range(tiles):
                nodes = slice(P * (first + tile_i), P * (first + tile_i + 1))
                for c in range(2):
                    a_codes, a_scales = live["aq", g, c]
                    feats = slice(F_HID * c, F_HID * (c + 1))
                    nc.tensor.matmul_mx(
                        out=bank[:, tile_i, :],
                        lhsT=a_codes[:, nodes].bitcast(FP8X4),
                        lhsT_scale=a_scales[:, nodes],
                        rhs=h_codes[:, feats].bitcast(FP8X4),
                        rhs_scale=h_scales[:, feats],
                        start=(c == 0),
                        stop=(c == 1),
                    )
            live["out_ps", g, first] = bank

        def add_bias(g, first, tiles):
            tile = out_pool.tile([P, tiles, F_HID], F32, name="out_sb")
            nc.vector.tensor_tensor(
                out=tile[:],
                in0=live["out_ps", g, first][:, 0:tiles, :],
                in1=bias[:].unsqueeze(1).to_broadcast([P, tiles, F_HID]),
                op=ALU.add,
            )
            live["out_sb", g, first] = tile

        def relu_store(g, first, tiles):
            tile = live["out_sb", g, first]
            nc.scalar.activation(out=tile[:], in_=tile[:], func=ACT.Relu)
            nc.sync.dma_start(
                out=out[g, P * first : P * (first + tiles), :].rearrange("(n p) f -> p n f", p=P), in_=tile[:]
            )

        load_adj(0, 2)
        load_adj(1, 4)
        load_x(0)
        load_adj(2, 4)
        load_x(1)
        bias = const.tile([P, F_HID], BF16)
        nc.sync.dma_start(out=bias[:], in_=b1.partition_broadcast(P))
        w_rows = const.tile([P, PACK, F_HID], BF16)
        nc.scalar.dma_start(
            out=w_rows[:].rearrange("q (u e) f -> q u (e f)", u=2),
            in_=W1.rearrange("(u q e) f -> q u (e f)", u=2, e=2),
        )
        ident = const.tile([P, P], F32)
        make_identity(nc, ident[:])
        ones = const.tile([P, 1], BF16)
        nc.vector.memset(ones[:], 1.0)
        tiny = const.tile([P, 1], F32)
        nc.vector.memset(tiny[:], TINY)
        first_root = const.tile([P, 1], F32)
        nc.scalar.activation(out=first_root[:], in_=tiny[:], func=ACT.Sqrt)
        w_grouped = const.tile([P, F_HID, PACK], BF16, align_bytes=64)
        nc.vector.tensor_copy(out=w_grouped[:], in_=w_rows[:].rearrange("q t f -> q f t"))
        w_codes = const.tile([P, F_HID], U32, align_bytes=64)
        w_scales = const.tile([P, F_HID], U8, align_bytes=64)
        nc.vector.quantize_mx(
            out=w_codes[:].bitcast(FP8X4), scales=w_scales[:], in_=w_grouped[:].rearrange("q f t -> q (f t)")
        )

        column_sums_in_parts(0, (4, 6, 8))
        root(0)
        invert_root(0)
        mask_r(0)
        scale_rows("scalar", 0, 0)
        scale_rows("vector", 0, 1)
        scale_rows("vector", 0, 2)
        scale_rows("vector", 0, 3)
        spread_gpsimd_r(0)
        spread_r(0)
        copy_gpsimd_r(0)
        column_sums(1, 0, ROW_TILES)

        for g in range(GRAPHS):
            first = g == 0
            last = g == GRAPHS - 1
            gpsimd_columns(g, 0)
            vector_columns(g, 0, 0)
            vector_columns(g, 0, 1)
            if last:
                copy_x(g, 0)
                copy_x(g, 1)
                scale_rows("scalar", g, 4)
                transpose_x(g, 2)
                transpose_x(g, 3)
                copy_x(g, 2)
                copy_x(g, 3)
                copy_h(g - 1, 0)
                copy_h(g - 1, 1)
                scale_rows("scalar", g, 5)
                scale_rows("scalar", g, 6)
                scale_rows("gpsimd", g, 7)
            else:
                scale_rows("scalar", g, 4)
                scale_rows("scalar", g, 5)
                if first:
                    scale_rows("scalar", g, 6)
                    scale_rows("vector", g, 7)
                root(g + 1)
                if first:
                    transpose_x(g, 0)
                    transpose_x(g, 1)
                else:
                    copy_h(g - 1, 0)
                    copy_h(g - 1, 1)
                copy_x(g, 0)
                copy_x(g, 1)
                if not first:
                    scale_rows("scalar", g, 6)
                    scale_rows("gpsimd", g, 7)
            if g + 1 < GRAPHS:
                invert_root(g + 1)
            if g >= 2:
                add_bias(g - 2, 4, 4)
                relu_store(g - 2, 4, 4)
            if g + 1 < GRAPHS:
                mask_r(g + 1)
                spread_gpsimd_r(g + 1)
            if last:
                quantise_x(g)
                quantise_a(g - 1, 1, 0, NODES)
                quantise_h(g - 1)
            elif not first:
                quantise_a(g - 1, 1, 0, NODES)
                quantise_h(g - 1)
            if last:
                matmul_h(g, 0)
                matmul_h(g, 1)
            else:
                transpose_x(g, 2)
                transpose_x(g, 3)
            if g + 2 < GRAPHS:
                load_x(g + 2)
            if g + 3 < GRAPHS:
                load_adj(g + 3, 4)
            if last:
                break
            if not first:
                matmul_out(g - 1, 0, 4)
                matmul_out(g - 1, 4, 4)
            gpsimd_columns(g, 1)
            vector_columns(g, 1, 0)
            vector_columns(g, 1, 1)
            scale_rows("scalar", g + 1, 0)
            copy_gpsimd_r(g + 1)
            if g + 2 < GRAPHS:
                column_sums(g + 2, 0, 4)
            copy_x(g, 2)
            copy_x(g, 3)
            scale_rows("scalar", g + 1, 1)
            scale_rows("scalar", g + 1, 2)
            scale_rows("gpsimd", g + 1, 3)
            if not first:
                add_bias(g - 1, 0, 4)
                relu_store(g - 1, 0, 4)
            spread_r(g + 1)
            if g + 2 < GRAPHS:
                column_sums(g + 2, 4, ROW_TILES)
            quantise_a(g, 0, 0, NODES)
            quantise_x(g)
            transpose_x(g + 1, 0)
            transpose_x(g + 1, 1)
            matmul_h(g, 0)
            matmul_h(g, 1)

        g = GRAPHS - 1
        matmul_out(g - 1, 0, 4)
        gpsimd_columns(g, 1)
        vector_columns(g, 1, 0)
        copy_h(g, 0)
        copy_h(g, 1)
        turn_rows(g, 1, 4)
        scale_turned(g, 4)
        turn_rows(g, 1, 5)
        scale_turned(g, 5)
        turn_back(g, 4)
        copy_turned(g, 1, 4)
        turn_back(g, 5)
        copy_turned(g, 1, 5)
        matmul_out(g - 1, 4, 4)
        add_bias(g - 1, 0, 4)
        relu_store(g - 1, 0, 4)
        quantise_a(g, 0, 0, NODES)
        quantise_h(g)
        quantise_a(g, 1, 0, HALF)
        matmul_out(g, 0, 4)
        add_bias(g - 1, 4, 4)
        relu_store(g - 1, 4, 4)
        quantise_a(g, 1, HALF, HALF + 2 * P)
        quantise_a(g, 1, HALF + 2 * P, NODES)
        matmul_out(g, 4, 2)
        add_bias(g, 0, 4)
        relu_store(g, 0, 4)
        matmul_out(g, 6, 2)
        add_bias(g, 4, 2)
        relu_store(g, 4, 2)
        add_bias(g, 6, 2)
        relu_store(g, 6, 2)
